import numpy as np
import ml_dtypes


def mxq(x, axis, fmt="e4m3"):
    dtype, down = {"e4m3": (ml_dtypes.float8_e4m3fn, 7), "e5m2": (ml_dtypes.float8_e5m2, 14)}[fmt]
    v = np.moveaxis(np.asarray(x, np.float32).astype(ml_dtypes.bfloat16).astype(np.float64), axis, -1)
    blocks = v.reshape(v.shape[:-1] + (-1, 32))
    amax = np.abs(blocks).max(-1, keepdims=True)
    byte = np.maximum(np.where(amax > 0, np.frexp(amax)[1] - 1 + 127, 0) - down, 1)
    scale = np.exp2(byte - 127.0)
    codes = (blocks / scale).astype(np.float32).astype(dtype).astype(np.float64)
    return np.moveaxis((codes * scale).reshape(v.shape), -1, axis)


WIDE = False


def mx_kscale(k):
    if not WIDE:
        return np.ones(k)
    levels = np.array([10, -10, 5, -5, 0])
    if k % 512:
        return np.exp2(np.random.permutation(np.resize(levels, k // 32))).repeat(32)
    a = np.empty((k // 512, 16))
    for p in range(k // 512):
        a[p, :8] = np.random.permutation(np.resize(levels, 8))
        for g in range(8):
            far = levels[np.abs(levels - a[p, g]) >= 10]
            a[p, g + 8] = far[np.random.randint(len(far))]
    return np.exp2(a.ravel()).repeat(32)


BF16 = ml_dtypes.bfloat16


def bf(x):
    return np.asarray(x, np.float32).astype(BF16)


def f64(x):
    return np.asarray(x).astype(np.float64)


B, O, A, H, Z = 4096, 512, 512, 512, 128
CLAMP = 10.0
LV_LO, LV_HI = -12.0, 2.0


def setup_inputs():
    s, t = mx_kscale(O + H), mx_kscale(H)
    return {
        "x_t": bf(np.random.standard_normal((B, O)) * s[:O]),
        "h_prev": bf(np.random.standard_normal((B, H)) * s[O:]),
        "eps": bf(np.random.standard_normal((B, Z))),
        "enc_w1": bf(np.random.standard_normal((H, O + H)) / np.sqrt(O + H) * t[:, None] / s[None, :]),
        "enc_b1": bf(np.random.standard_normal(H) * 0.1 * t),
        "enc_w2": bf(np.random.standard_normal((2 * Z, H)) * 1.4 / np.sqrt(H) / t[None, :]),
        "enc_b2": bf(np.concatenate([np.random.standard_normal(Z) * 0.1, np.random.uniform(LV_LO, LV_HI, Z)])),
        "mu_p": bf(np.random.standard_normal((B, Z)) * 0.7),
        "logvar_p": bf(np.random.standard_normal((B, Z)) * 0.7),
    }


def reference(x_t, h_prev, eps, enc_w1, enc_b1, enc_w2, enc_b2, mu_p, logvar_p):
    mu_p, logvar_p = f64(mu_p), f64(logvar_p)
    xh = np.concatenate([f64(x_t), f64(h_prev)], -1)
    hid = np.maximum((mxq(xh, 1, "e4m3") @ mxq(f64(enc_w1), 1, "e4m3").T) + f64(enc_b1), 0.0)
    stats = (mxq(hid, 1, "e4m3") @ mxq(f64(enc_w2), 1, "e4m3").T) + f64(enc_b2)
    mu_q = stats[:, :Z]
    logvar_q = np.clip(stats[:, Z:], -CLAMP, CLAMP)
    std_q = np.exp(0.5 * logvar_q)
    z_t = mu_q + f64(eps) * std_q
    var_p = np.exp(logvar_p)
    kl = 0.5 * np.sum((mu_q - mu_p) ** 2 / var_p + np.exp(logvar_q) / var_p + (logvar_p - logvar_q) - 1.0, axis=-1)
    return z_t, mu_q, logvar_q, kl

@@ -1,0 +1,371 @@
+from contextlib import ExitStack
+
+import concourse.mybir as mybir
+from concourse.masks import make_identity
+
+F32 = mybir.dt.float32
+BF16 = mybir.dt.bfloat16
+U32 = mybir.dt.uint32
+U8 = mybir.dt.uint8
+FP8X4 = mybir.dt.float8_e4m3fn_x4
+ACT = mybir.ActivationFunctionType
+ALU = mybir.AluOpType
+
+P = 128
+B, O, H, Z = 4096, 512, 512, 128
+CLAMP = 10.0
+PACK = 4
+K_PASS = P * PACK
+WORDS = K_PASS // 2
+TILES = B // P
+TPC = 4
+CHUNK = TPC * P
+NCH = TILES // TPC
+HALF_TILES = TILES // 2
+H_TILES = H // P
+
+VECTOR_COPIES = 1
+LEAD = 3
+
+FLOPS = 2 * B * (O + H) * H + 2 * B * H * 2 * Z
+
+
+def transpose_words(nc, bank, ident, word_blocks):
+    for s in range(2):
+        for u in range(2):
+            nc.tensor.transpose(bank[:, u, s * P : (s + 1) * P], word_blocks[s][u], ident)
+
+
+def copy_grouped(copy, bank, grouped_words):
+    copy(out=grouped_words.rearrange("p (c u) -> p c u", u=2), in_=bank.rearrange("p u c -> p c u"))
+
+
+def tile_vrnncell_pa_t_kernel(
+    tc, x_t, h_prev, eps, enc_w1, enc_b1, enc_w2, enc_b2, mu_p, logvar_p, z_out, mu_out, lv_out, kl_out
+):
+    nc = tc.nc
+    with ExitStack() as ctx:
+        ctx.enter_context(tc.manual_schedule())
+        const = ctx.enter_context(tc.tile_pool(name="const", bufs=1))
+        resident = ctx.enter_context(tc.tile_pool(name="resident", bufs=NCH))
+        prior = ctx.enter_context(tc.tile_pool(name="prior", bufs=2))
+        xq = ctx.enter_context(tc.tile_pool(name="xq", bufs=2))
+        hq = ctx.enter_context(tc.tile_pool(name="hq", bufs=2))
+        outp = ctx.enter_context(tc.tile_pool(name="outp", bufs=3))
+        scr = ctx.enter_context(tc.tile_pool(name="scr", bufs=2))
+        psum_t = ctx.enter_context(tc.psum_pool(name="psum_t", bufs=LEAD))
+        psum_h = ctx.enter_context(tc.psum_pool(name="psum_h", bufs=LEAD))
+        psum_s = ctx.enter_context(tc.psum_pool(name="psum_s", bufs=1))
+
+        def by_tile(dram):
+            return dram.rearrange("(p j) z -> p j z", j=TILES)
+
+        def live(c):
+            return 0 <= c < NCH
+
+        x_sb = []
+        h_sb = []
+
+        def load_chunk(c):
+            tiles = slice(c * TPC, (c + 1) * TPC)
+            x_in = resident.tile([P, TPC * O], BF16, name="x_in")
+            nc.sync.dma_start(out=x_in.rearrange("p (j k) -> p j k", j=TPC), in_=by_tile(x_t)[:, tiles, :])
+            h_in = resident.tile([P, TPC * H], BF16, name="h_in")
+            nc.sync.dma_start(out=h_in.rearrange("p (j k) -> p j k", j=TPC), in_=by_tile(h_prev)[:, tiles, :])
+            x_sb.append(x_in)
+            h_sb.append(h_in)
+
+        eps_sb = []
+        mup_sb = []
+        lvp_sb = []
+
+        def load_prior(half):
+            tiles = slice(half * HALF_TILES, (half + 1) * HALF_TILES)
+            for dram, keep, label in ((logvar_p, lvp_sb, "lvp"), (mu_p, mup_sb, "mup"), (eps, eps_sb, "eps")):
+                t = prior.tile([P, HALF_TILES, Z], BF16, name=label)
+                nc.sync.dma_start(out=t, in_=by_tile(dram)[:, tiles, :])
+                keep.append(t)
+
+        def of_chunk(halves, c):
+            first = (c * TPC) % HALF_TILES
+            return halves[(c * TPC) // HALF_TILES][:, first : first + TPC, :]
+
+        w1_sb = const.tile([P, H_TILES * (O + H)], BF16, name="w1_sb")
+        nc.sync.dma_start(
+            out=w1_sb.rearrange("p (t k) -> p t k", t=H_TILES),
+            in_=enc_w1.rearrange("(p t) k -> p t k", t=H_TILES),
+        )
+        load_chunk(0)
+        w2_sb = const.tile([P, 2 * H], BF16, name="w2_sb")
+        nc.scalar.dma_start(
+            out=w2_sb.rearrange("p (a k) -> p a k", a=2), in_=enc_w2.rearrange("(a p) k -> p a k", p=P)
+        )
+        b1_sb = const.tile([P, H_TILES], BF16, name="b1_sb")
+        nc.scalar.dma_start(out=b1_sb, in_=enc_b1.rearrange("(p t) -> p t", t=H_TILES))
+        b2_bc = const.tile([P, 2 * Z], BF16, name="b2_bc")
+        nc.scalar.dma_start(out=b2_bc, in_=enc_b2.partition_broadcast(P))
+        load_chunk(1)
+        load_prior(0)
+        for c in range(2, NCH // 2 + 1):
+            load_chunk(c)
+        load_prior(1)
+        for c in range(NCH // 2 + 1, NCH):
+            load_chunk(c)
+
+        ident = const.tile([P, P], F32, name="ident")
+        make_identity(nc, ident)
+
+        w1_words = w1_sb.bitcast(F32)
+        w1_g = const.tile([P, 2 * H_TILES * P * PACK], BF16, name="w1_g", align_bytes=64)
+        w1_g_words = w1_g.bitcast(F32)
+        for g in range(2):
+            for a in range(2):
+                starts = [(2 * a + s) * 2 * WORDS + g * WORDS for s in range(2)]
+                bank = psum_t.tile([P, 2, 2 * P], F32, name="bank")
+                transpose_words(nc, bank, ident, [[w1_words[:, w + u : w + WORDS : 2] for u in range(2)] for w in starts])
+                first = (g * H_TILES + 2 * a) * 2 * P
+                copy = nc.vector.tensor_copy if a == 0 else nc.scalar.copy
+                copy_grouped(copy, bank, w1_g_words[:, first : first + 4 * P])
+        w1_c = const.tile([P, 2 * H_TILES * P], U32, name="w1_c", align_bytes=64)
+        w1_s = const.tile([P, 2 * H_TILES * P], U8, name="w1_s", align_bytes=64)
+        nc.vector.quantize_mx(out=w1_c.bitcast(FP8X4), scales=w1_s, in_=w1_g)
+        b1_f = const.tile([P, H_TILES], F32, name="b1_f")
+        nc.vector.tensor_copy(out=b1_f, in_=b1_sb)
+
+        banks = {}
+        x_g = {}
+        x_q = {}
+
+        def fill_bank(n):
+            c, g, a = n // 4, (n % 4) // 2, n % 2
+            src_words = (x_sb[c], h_sb[c])[g].bitcast(F32)
+            starts = [(2 * a + s) * WORDS for s in range(2)]
+            banks[n] = psum_t.tile([P, 2, 2 * P], F32, name="bank")
+            transpose_words(
+                nc, banks[n], ident, [[src_words[:, w + u : w + WORDS : 2] for u in range(2)] for w in starts]
+            )
+
+        def empty_bank(n):
+            c = n // 4
+            if n % 4 == 0:
+                x_g[c] = xq.tile([P, 2 * CHUNK * PACK], BF16, name="x_g", align_bytes=64)
+            first = (n % 4) * 4 * P
+            copy = nc.vector.tensor_copy if n % 4 < VECTOR_COPIES else nc.scalar.copy
+            copy_grouped(copy, banks[n], x_g[c].bitcast(F32)[:, first : first + 4 * P])
+
+        def quantise_inputs(c):
+            codes = xq.tile([P, 2 * CHUNK], U32, name="x_codes", align_bytes=64)
+            scales = xq.tile([P, 2 * CHUNK], U8, name="x_scales", align_bytes=64)
+            for g in range(2):
+                cols = slice(g * CHUNK, (g + 1) * CHUNK)
+                nc.vector.quantize_mx(
+                    out=codes[:, cols].bitcast(FP8X4),
+                    scales=scales[:, cols],
+                    in_=x_g[c][:, g * CHUNK * PACK : (g + 1) * CHUNK * PACK],
+                )
+            x_q[c] = (codes, scales)
+
+        accs = {}
+        h_b = {}
+        h_g = {}
+        h_q = {}
+
+        def hidden_group(c, t):
+            codes, scales = x_q[c]
+            accs[(c, t)] = psum_h.tile([P, CHUNK], F32, name="acc")
+            for g in range(2):
+                w_cols = slice((g * H_TILES + t) * P, (g * H_TILES + t + 1) * P)
+                x_cols = slice(g * CHUNK, (g + 1) * CHUNK)
+                nc.tensor.matmul_mx(
+                    out=accs[(c, t)],
+                    lhsT=w1_c[:, w_cols].bitcast(FP8X4),
+                    lhsT_scale=w1_s[:, w_cols],
+                    rhs=codes[:, x_cols].bitcast(FP8X4),
+                    rhs_scale=scales[:, x_cols],
+                    start=(g == 0),
+                    stop=(g == 1),
+                )
+
+        def relu_group(c, t):
+            if t == 0:
+                h_b[c] = hq.tile([P, H_TILES, CHUNK], BF16, name="h_b")
+            nc.scalar.activation(out=h_b[c][:, t, :], in_=accs[(c, t)], func=ACT.Relu, bias=b1_f[:, t : t + 1])
+
+        def regroup_hidden(c):
+            h_g[c] = hq.tile([P, CHUNK * PACK], BF16, name="h_g", align_bytes=64)
+            nc.vector.tensor_copy(
+                out=h_g[c].rearrange("p (c i t) -> p c t i", i=4, t=PACK),
+                in_=h_b[c].rearrange("p t (c i) -> p c t i", i=4),
+            )
+
+        def quantise_hidden(c):
+            codes = hq.tile([P, CHUNK], U32, name="h_codes", align_bytes=64)
+            scales = hq.tile([P, CHUNK], U8, name="h_scales", align_bytes=64)
+            nc.vector.quantize_mx(out=codes.bitcast(FP8X4), scales=scales, in_=h_g[c])
+            h_q[c] = (codes, scales)
+
+        st_mu = {}
+        st_lv = {}
+
+        def stats_matmuls(c):
+            codes, scales = h_q[c]
+            st_mu[c] = psum_s.tile([P, TPC, Z], F32, name="st_mu")
+            st_lv[c] = psum_s.tile([P, TPC, Z], F32, name="st_lv")
+            for j in range(TPC):
+                tok = slice(j * P, (j + 1) * P)
+                for part, dst in enumerate((st_mu[c], st_lv[c])):
+                    cols = slice(part * Z, (part + 1) * Z)
+                    nc.tensor.matmul_mx(
+                        out=dst[:, j, :],
+                        lhsT=codes[:, tok].bitcast(FP8X4),
+                        lhsT_scale=scales[:, tok],
+                        rhs=w2_c[:, cols].bitcast(FP8X4),
+                        rhs_scale=w2_s[:, cols],
+                        start=True,
+                        stop=True,
+                    )
+
+        def chunk_tile(pool, label, dtype=F32):
+            return pool.tile([P, TPC, Z], dtype, name=label)
+
+        def store(dram, c, tile):
+            nc.sync.dma_start(out=by_tile(dram)[:, c * TPC : (c + 1) * TPC, :], in_=tile)
+
+        def bias_of(part):
+            return b2_bc[:, part * Z : (part + 1) * Z].unsqueeze(1).to_broadcast([P, TPC, Z])
+
+        mu = {}
+        lv_raw = {}
+        lv = {}
+        std = {}
+        inv_sd_p = {}
+        diff = {}
+        ratio = {}
+        dlv = {}
+        noise = {}
+        sum_sq = const.tile([P, TILES], F32, name="sum_sq")
+        sum_ex = const.tile([P, TILES], F32, name="sum_ex")
+        sum_df = const.tile([P, TILES], F32, name="sum_df")
+
+        def add_bias_mean(c):
+            mu[c] = chunk_tile(outp, "mu")
+            nc.vector.tensor_tensor(out=mu[c], in0=st_mu[c], in1=bias_of(0), op=ALU.add)
+            store(mu_out, c, mu[c])
+
+        def add_bias_logvar(c):
+            lv_raw[c] = chunk_tile(scr, "lv_raw")
+            nc.vector.tensor_tensor(out=lv_raw[c], in0=st_lv[c], in1=bias_of(1), op=ALU.add)
+
+        def clip_logvar(c):
+            lv[c] = chunk_tile(outp, "lv")
+            nc.vector.tensor_scalar(
+                out=lv[c], in0=lv_raw[c], scalar1=-CLAMP, scalar2=CLAMP, op0=ALU.max, op1=ALU.min
+            )
+            store(lv_out, c, lv[c])
+
+        def mean_difference(c):
+            diff[c] = chunk_tile(scr, "diff")
+            nc.vector.tensor_tensor(out=diff[c], in0=mu[c], in1=of_chunk(mup_sb, c), op=ALU.subtract)
+
+        def scale_difference(c):
+            ratio[c] = chunk_tile(scr, "ratio")
+            nc.vector.tensor_tensor(out=ratio[c], in0=diff[c], in1=inv_sd_p[c], op=ALU.mult)
+
+        def logvar_difference(c):
+            dlv[c] = chunk_tile(scr, "dlv")
+            for j in range(TPC):
+                nc.vector.scalar_tensor_tensor(
+                    out=dlv[c][:, j, :],
+                    in0=lv[c][:, j, :],
+                    scalar=1.0,
+                    in1=of_chunk(lvp_sb, c)[:, j, :],
+                    op0=ALU.mult,
+                    op1=ALU.subtract,
+                    accum_out=sum_df[:, c * TPC + j : c * TPC + j + 1],
+                )
+
+        def posterior_sd(c):
+            std[c] = chunk_tile(scr, "std")
+            nc.scalar.activation(out=std[c], in_=lv[c], func=ACT.Exp, scale=0.5)
+
+        def prior_inverse_sd(c):
+            inv_sd_p[c] = chunk_tile(scr, "inv_sd_p")
+            nc.scalar.activation(out=inv_sd_p[c], in_=of_chunk(lvp_sb, c), func=ACT.Exp, scale=-0.5)
+
+        def row_sums(c, func, values, sums, label):
+            unread = chunk_tile(scr, label, BF16)
+            for j in range(TPC):
+                nc.scalar.activation(
+                    out=unread[:, j, :],
+                    in_=values[:, j, :],
+                    func=func,
+                    accum_out=sums[:, c * TPC + j : c * TPC + j + 1],
+                )
+
+        def scale_noise(c):
+            noise[c] = chunk_tile(scr, "noise")
+            nc.vector.tensor_tensor(out=noise[c], in0=std[c], in1=of_chunk(eps_sb, c), op=ALU.mult)
+
+        def add_mean(c):
+            z = chunk_tile(outp, "z")
+            nc.vector.tensor_tensor(out=z, in0=noise[c], in1=mu[c], op=ALU.add)
+            store(z_out, c, z)
+
+        for n in range(LEAD):
+            fill_bank(n)
+
+        w2_words = w2_sb.bitcast(F32).rearrange("p (a w u) -> p a u w", a=2, u=2)
+        w2_g = const.tile([P, 2 * Z * PACK], BF16, name="w2_g", align_bytes=64)
+        w2_bank = psum_s.tile([P, 2, 2 * P], F32, name="w2_bank", tag="st_mu")
+        transpose_words(nc, w2_bank, ident, [[w2_words[:, a, u, :] for u in range(2)] for a in range(2)])
+        copy_grouped(nc.vector.tensor_copy, w2_bank, w2_g.bitcast(F32))
+        w2_c = const.tile([P, 2 * Z], U32, name="w2_c", align_bytes=64)
+        w2_s = const.tile([P, 2 * Z], U8, name="w2_s", align_bytes=64)
+        nc.vector.quantize_mx(out=w2_c.bitcast(FP8X4), scales=w2_s, in_=w2_g)
+
+        for i in range(NCH + 3):
+            if live(i - 1):
+                for t in range(H_TILES):
+                    relu_group(i - 1, t)
+                    if t + LEAD < H_TILES:
+                        hidden_group(i - 1, t + LEAD)
+            if live(i - 2):
+                add_bias_logvar(i - 2)
+                add_bias_mean(i - 2)
+                clip_logvar(i - 2)
+                mean_difference(i - 2)
+                logvar_difference(i - 2)
+                scale_difference(i - 2)
+            if live(i):
+                for q in range(4):
+                    empty_bank(4 * i + q)
+                    if 4 * i + q + LEAD < 4 * NCH:
+                        fill_bank(4 * i + q + LEAD)
+            if live(i - 1):
+                regroup_hidden(i - 1)
+            if live(i - 3):
+                scale_noise(i - 3)
+            if live(i - 1):
+                quantise_hidden(i - 1)
+                stats_matmuls(i - 1)
+            if live(i - 3):
+                add_mean(i - 3)
+            if live(i):
+                quantise_inputs(i)
+                for t in range(LEAD):
+                    hidden_group(i, t)
+            if live(i - 2):
+                posterior_sd(i - 2)
+            if live(i - 1):
+                prior_inverse_sd(i - 1)
+            if live(i - 2):
+                row_sums(i - 2, ACT.Exp, dlv[i - 2], sum_ex, "ex_unread")
+                row_sums(i - 2, ACT.Square, ratio[i - 2], sum_sq, "sq_unread")
+
+        total = const.tile([P, TILES], F32, name="total")
+        nc.vector.tensor_tensor(out=total, in0=sum_sq, in1=sum_ex, op=ALU.add)
+        total2 = const.tile([P, TILES], F32, name="total2")
+        nc.vector.tensor_tensor(out=total2, in0=total, in1=sum_df, op=ALU.subtract)
+        kl = const.tile([P, TILES], F32, name="kl")
+        nc.vector.tensor_scalar(out=kl, in0=total2, scalar1=0.5, scalar2=-0.5 * Z, op0=ALU.mult, op1=ALU.add)
+        nc.sync.dma_start(out=kl_out.rearrange("(p j) -> p j", j=TILES), in_=kl)

@@ -90,6 +90,11 @@ def tile_vrnncell_pa_t_kernel(
             first = (c * TPC) % HALF_TILES
             return halves[(c * TPC) // HALF_TILES][:, first : first + TPC, :]
 
+        b2_row = const.tile([P, 2 * Z], BF16, name="b2_row")
+        nc.gpsimd.memset(b2_row, 0.0)
+        ones = const.tile([P, P], BF16, name="ones")
+        nc.gpsimd.memset(ones, 1.0)
+
         w1_sb = const.tile([P, H_TILES * (O + H)], BF16, name="w1_sb")
         nc.sync.dma_start(
             out=w1_sb.rearrange("p (t k) -> p t k", t=H_TILES),
@@ -102,8 +107,7 @@ def tile_vrnncell_pa_t_kernel(
         )
         b1_sb = const.tile([P, H_TILES], BF16, name="b1_sb")
         nc.scalar.dma_start(out=b1_sb, in_=enc_b1.rearrange("(p t) -> p t", t=H_TILES))
-        b2_bc = const.tile([P, 2 * Z], BF16, name="b2_bc")
-        nc.scalar.dma_start(out=b2_bc, in_=enc_b2.partition_broadcast(P))
+        nc.scalar.dma_start(out=b2_row[0:1, :], in_=enc_b2.rearrange("(a z) -> a z", a=1))
         load_chunk(1)
         load_prior(0)
         for c in range(2, NCH // 2 + 1):
@@ -322,6 +326,10 @@ def tile_vrnncell_pa_t_kernel(
         w2_c = const.tile([P, 2 * Z], U32, name="w2_c", align_bytes=64)
         w2_s = const.tile([P, 2 * Z], U8, name="w2_s", align_bytes=64)
         nc.vector.quantize_mx(out=w2_c.bitcast(FP8X4), scales=w2_s, in_=w2_g)
+        b2_bank = psum_s.tile([P, 2 * Z], F32, name="b2_bank", tag="st_lv")
+        nc.tensor.matmul(b2_bank, lhsT=ones, rhs=b2_row, start=True, stop=True)
+        b2_bc = const.tile([P, 2 * Z], F32, name="b2_bc")
+        nc.vector.tensor_copy(out=b2_bc, in_=b2_bank)
 
         for i in range(NCH + 3):
             if live(i - 1):

@@ -18,22 +18,21 @@ PACK = 4
 K_PASS = P * PACK
 WORDS = K_PASS // 2
 TILES = B // P
-TPC = 4
-CHUNK = TPC * P
-NCH = TILES // TPC
-HALF_TILES = TILES // 2
 H_TILES = H // P
 
-VECTOR_COPIES = 1
+CHUNKS = (2, 2, 4, 4, 4, 4, 4, 4, 2, 2)
+FIRST = tuple(sum(CHUNKS[:c]) for c in range(len(CHUNKS)))
+NCH = len(CHUNKS)
+MAX_N = max(CHUNKS)
 LEAD = 3
 
 FLOPS = 2 * B * (O + H) * H + 2 * B * H * 2 * Z
 
 
-def transpose_words(nc, bank, ident, word_blocks):
-    for s in range(2):
+def transpose_words(nc, bank, ident, blocks):
+    for s, words in enumerate(blocks):
         for u in range(2):
-            nc.tensor.transpose(bank[:, u, s * P : (s + 1) * P], word_blocks[s][u], ident)
+            nc.tensor.transpose(bank[:, u, s * P : (s + 1) * P], words[:, u:WORDS:2], ident)
 
 
 def copy_grouped(copy, bank, grouped_words):
@@ -48,7 +47,6 @@ def tile_vrnncell_pa_t_kernel(
         ctx.enter_context(tc.manual_schedule())
         const = ctx.enter_context(tc.tile_pool(name="const", bufs=1))
         resident = ctx.enter_context(tc.tile_pool(name="resident", bufs=NCH))
-        prior = ctx.enter_context(tc.tile_pool(name="prior", bufs=2))
         xq = ctx.enter_context(tc.tile_pool(name="xq", bufs=2))
         hq = ctx.enter_context(tc.tile_pool(name="hq", bufs=2))
         outp = ctx.enter_context(tc.tile_pool(name="outp", bufs=3))
@@ -60,186 +58,214 @@ def tile_vrnncell_pa_t_kernel(
         def by_tile(dram):
             return dram.rearrange("(p j) z -> p j z", j=TILES)
 
-        def live(c):
-            return 0 <= c < NCH
-
-        x_sb = []
-        h_sb = []
-
-        def load_chunk(c):
-            tiles = slice(c * TPC, (c + 1) * TPC)
-            x_in = resident.tile([P, TPC * O], BF16, name="x_in")
-            nc.sync.dma_start(out=x_in.rearrange("p (j k) -> p j k", j=TPC), in_=by_tile(x_t)[:, tiles, :])
-            h_in = resident.tile([P, TPC * H], BF16, name="h_in")
-            nc.sync.dma_start(out=h_in.rearrange("p (j k) -> p j k", j=TPC), in_=by_tile(h_prev)[:, tiles, :])
-            x_sb.append(x_in)
-            h_sb.append(h_in)
-
-        eps_sb = []
-        mup_sb = []
-        lvp_sb = []
-
-        def load_prior(half):
-            tiles = slice(half * HALF_TILES, (half + 1) * HALF_TILES)
-            for dram, keep, label in ((logvar_p, lvp_sb, "lvp"), (mu_p, mup_sb, "mup"), (eps, eps_sb, "eps")):
-                t = prior.tile([P, HALF_TILES, Z], BF16, name=label)
-                nc.sync.dma_start(out=t, in_=by_tile(dram)[:, tiles, :])
-                keep.append(t)
-
-        def of_chunk(halves, c):
-            first = (c * TPC) % HALF_TILES
-            return halves[(c * TPC) // HALF_TILES][:, first : first + TPC, :]
+        def tiles_of(c):
+            return slice(FIRST[c], FIRST[c] + CHUNKS[c])
 
         b2_row = const.tile([P, 2 * Z], BF16, name="b2_row")
         nc.gpsimd.memset(b2_row, 0.0)
         ones = const.tile([P, P], BF16, name="ones")
         nc.gpsimd.memset(ones, 1.0)
-
-        w1_sb = const.tile([P, H_TILES * (O + H)], BF16, name="w1_sb")
-        nc.sync.dma_start(
-            out=w1_sb.rearrange("p (t k) -> p t k", t=H_TILES),
-            in_=enc_w1.rearrange("(p t) k -> p t k", t=H_TILES),
-        )
-        load_chunk(0)
-        w2_sb = const.tile([P, 2 * H], BF16, name="w2_sb")
-        nc.scalar.dma_start(
-            out=w2_sb.rearrange("p (a k) -> p a k", a=2), in_=enc_w2.rearrange("(a p) k -> p a k", p=P)
-        )
-        b1_sb = const.tile([P, H_TILES], BF16, name="b1_sb")
-        nc.scalar.dma_start(out=b1_sb, in_=enc_b1.rearrange("(p t) -> p t", t=H_TILES))
-        nc.scalar.dma_start(out=b2_row[0:1, :], in_=enc_b2.rearrange("(a z) -> a z", a=1))
-        load_chunk(1)
-        load_prior(0)
-        for c in range(2, NCH // 2 + 1):
-            load_chunk(c)
-        load_prior(1)
-        for c in range(NCH // 2 + 1, NCH):
-            load_chunk(c)
-
         ident = const.tile([P, P], F32, name="ident")
         make_identity(nc, ident)
 
-        w1_words = w1_sb.bitcast(F32)
+        xh_sb = []
+
+        def load_chunk(c):
+            pair = []
+            for dram, label in ((x_t, "x_in"), (h_prev, "h_in")):
+                t = resident.tile([P, CHUNKS[c] * O], BF16, name=label)
+                nc.sync.dma_start(
+                    out=t.rearrange("p (j k) -> p j k", j=CHUNKS[c]), in_=by_tile(dram)[:, tiles_of(c), :]
+                )
+                pair.append(t)
+            xh_sb.append(pair)
+
+        eps_sb = const.tile([P, TILES, Z], BF16, name="eps_sb")
+        mup_sb = const.tile([P, TILES, Z], BF16, name="mup_sb")
+        lvp_sb = const.tile([P, TILES, Z], BF16, name="lvp_sb")
+
+        def load_prior(chunks):
+            tiles = slice(tiles_of(chunks[0]).start, tiles_of(chunks[-1]).stop)
+            for dram, t in ((logvar_p, lvp_sb), (mu_p, mup_sb), (eps, eps_sb)):
+                nc.sync.dma_start(out=t[:, tiles, :], in_=by_tile(dram)[:, tiles, :])
+
+        load_chunk(0)
+        w1_sb = const.tile([P, H_TILES * (O + H)], BF16, name="w1_sb")
+        for a in range(2):
+            rows = slice(2 * a, 2 * a + 2)
+            nc.sync.dma_start(
+                out=w1_sb.rearrange("p (t k) -> p t k", t=H_TILES)[:, rows, :],
+                in_=enc_w1.rearrange("(p t) k -> p t k", t=H_TILES)[:, rows, :],
+            )
+        b1_sb = const.tile([P, H_TILES], BF16, name="b1_sb")
+        nc.scalar.dma_start(out=b1_sb, in_=enc_b1.rearrange("(p t) -> p t", t=H_TILES))
+        nc.scalar.dma_start(out=b2_row[0:1, :], in_=enc_b2.rearrange("(a z) -> a z", a=1))
+        w2_sb = const.tile([P, 2 * H], BF16, name="w2_sb")
+        nc.sync.dma_start(
+            out=w2_sb.rearrange("p (a k) -> p a k", a=2), in_=enc_w2.rearrange("(a p) k -> p a k", p=P)
+        )
+        load_chunk(1)
+        load_prior(range(0, 2))
+        load_chunk(2)
+        load_chunk(3)
+        load_prior(range(2, 5))
+        for c in range(4, 6):
+            load_chunk(c)
+        load_prior(range(5, NCH))
+        for c in range(6, NCH):
+            load_chunk(c)
+
         w1_g = const.tile([P, 2 * H_TILES * P * PACK], BF16, name="w1_g", align_bytes=64)
-        w1_g_words = w1_g.bitcast(F32)
-        for g in range(2):
-            for a in range(2):
-                starts = [(2 * a + s) * 2 * WORDS + g * WORDS for s in range(2)]
-                bank = psum_t.tile([P, 2, 2 * P], F32, name="bank")
-                transpose_words(nc, bank, ident, [[w1_words[:, w + u : w + WORDS : 2] for u in range(2)] for w in starts])
-                first = (g * H_TILES + 2 * a) * 2 * P
-                copy = nc.vector.tensor_copy if a == 0 else nc.scalar.copy
-                copy_grouped(copy, bank, w1_g_words[:, first : first + 4 * P])
         w1_c = const.tile([P, 2 * H_TILES * P], U32, name="w1_c", align_bytes=64)
         w1_s = const.tile([P, 2 * H_TILES * P], U8, name="w1_s", align_bytes=64)
-        nc.vector.quantize_mx(out=w1_c.bitcast(FP8X4), scales=w1_s, in_=w1_g)
-        b1_f = const.tile([P, H_TILES], F32, name="b1_f")
-        nc.vector.tensor_copy(out=b1_f, in_=b1_sb)
-
-        banks = {}
         x_g = {}
         x_q = {}
 
-        def fill_bank(n):
-            c, g, a = n // 4, (n % 4) // 2, n % 2
-            src_words = (x_sb[c], h_sb[c])[g].bitcast(F32)
-            starts = [(2 * a + s) * WORDS for s in range(2)]
-            banks[n] = psum_t.tile([P, 2, 2 * P], F32, name="bank")
-            transpose_words(
-                nc, banks[n], ident, [[src_words[:, w + u : w + WORDS : 2] for u in range(2)] for w in starts]
+        def chunk_fills(c):
+            blocks = [xh_sb[c][g].bitcast(F32)[:, j * WORDS : (j + 1) * WORDS] for g in range(2) for j in range(CHUNKS[c])]
+            return [(blocks[2 * q : 2 * q + 2], c, q) for q in range(CHUNKS[c])]
+
+        def weight_fills():
+            words = w1_sb.bitcast(F32)
+            found = []
+            for a in range(2):
+                for g in range(2):
+                    starts = [((2 * a + s) * 2 + g) * WORDS for s in range(2)]
+                    found.append(([words[:, w : w + WORDS] for w in starts], None, 2 * a + g))
+            return found
+
+        fills = chunk_fills(0) + weight_fills()
+        for c in range(1, NCH):
+            fills = fills + chunk_fills(c)
+        banks = []
+
+        def fill_next():
+            if len(banks) < len(fills):
+                bank = psum_t.tile([P, 2, 2 * P], F32, name="bank")
+                transpose_words(nc, bank, ident, fills[len(banks)][0])
+                banks.append(bank)
+
+        emptied = []
+
+        def empty_next(copy, refill=True):
+            n = len(emptied)
+            c, q = fills[n][1:]
+            if c is None:
+                grouped = w1_g
+            else:
+                if q == 0:
+                    x_g[c] = xq.tile([P, 2 * CHUNKS[c] * P * PACK], BF16, name="x_g", align_bytes=64)
+                grouped = x_g[c]
+            copy_grouped(copy, banks[n], grouped.bitcast(F32)[:, q * 4 * P : (q + 1) * 4 * P])
+            emptied.append(n)
+            if refill:
+                fill_next()
+
+        def quantise_w1(a):
+            cols = slice(a * 4 * P, (a + 1) * 4 * P)
+            nc.vector.quantize_mx(
+                out=w1_c[:, cols].bitcast(FP8X4),
+                scales=w1_s[:, cols],
+                in_=w1_g[:, a * 4 * P * PACK : (a + 1) * 4 * P * PACK],
             )
 
-        def empty_bank(n):
-            c = n // 4
-            if n % 4 == 0:
-                x_g[c] = xq.tile([P, 2 * CHUNK * PACK], BF16, name="x_g", align_bytes=64)
-            first = (n % 4) * 4 * P
-            copy = nc.vector.tensor_copy if n % 4 < VECTOR_COPIES else nc.scalar.copy
-            copy_grouped(copy, banks[n], x_g[c].bitcast(F32)[:, first : first + 4 * P])
-
         def quantise_inputs(c):
-            codes = xq.tile([P, 2 * CHUNK], U32, name="x_codes", align_bytes=64)
-            scales = xq.tile([P, 2 * CHUNK], U8, name="x_scales", align_bytes=64)
-            for g in range(2):
-                cols = slice(g * CHUNK, (g + 1) * CHUNK)
-                nc.vector.quantize_mx(
-                    out=codes[:, cols].bitcast(FP8X4),
-                    scales=scales[:, cols],
-                    in_=x_g[c][:, g * CHUNK * PACK : (g + 1) * CHUNK * PACK],
-                )
+            width = 2 * CHUNKS[c] * P
+            codes = xq.tile([P, width], U32, name="x_codes", align_bytes=64)
+            scales = xq.tile([P, width], U8, name="x_scales", align_bytes=64)
+            nc.vector.quantize_mx(out=codes.bitcast(FP8X4), scales=scales, in_=x_g[c])
             x_q[c] = (codes, scales)
 
         accs = {}
+        h_banks = []
         h_b = {}
         h_g = {}
         h_q = {}
 
-        def hidden_group(c, t):
+        def per_bank(c):
+            return MAX_N // CHUNKS[c]
+
+        def hidden_banks(c):
+            return H_TILES // per_bank(c)
+
+        def hidden_bank(c, b):
             codes, scales = x_q[c]
-            accs[(c, t)] = psum_h.tile([P, CHUNK], F32, name="acc")
-            for g in range(2):
-                w_cols = slice((g * H_TILES + t) * P, (g * H_TILES + t + 1) * P)
-                x_cols = slice(g * CHUNK, (g + 1) * CHUNK)
-                nc.tensor.matmul_mx(
-                    out=accs[(c, t)],
-                    lhsT=w1_c[:, w_cols].bitcast(FP8X4),
-                    lhsT_scale=w1_s[:, w_cols],
-                    rhs=codes[:, x_cols].bitcast(FP8X4),
-                    rhs_scale=scales[:, x_cols],
-                    start=(g == 0),
-                    stop=(g == 1),
+            tokens = CHUNKS[c] * P
+            accs[(c, b)] = psum_h.tile([P, per_bank(c), tokens], F32, name="acc")
+            for i in range(per_bank(c)):
+                a, s = divmod(b * per_bank(c) + i, 2)
+                for g in range(2):
+                    w_first = ((2 * a + g) * 2 + s) * P
+                    w_cols = slice(w_first, w_first + P)
+                    x_cols = slice(g * tokens, (g + 1) * tokens)
+                    nc.tensor.matmul_mx(
+                        out=accs[(c, b)][:, i, :],
+                        lhsT=w1_c[:, w_cols].bitcast(FP8X4),
+                        lhsT_scale=w1_s[:, w_cols],
+                        rhs=codes[:, x_cols].bitcast(FP8X4),
+                        rhs_scale=scales[:, x_cols],
+                        start=(g == 0),
+                        stop=(g == 1),
+                    )
+
+        hidden_order = [(c, b) for c in range(NCH) for b in range(hidden_banks(c))]
+
+        def fill_hidden():
+            first = len(accs)
+            last = min(len(h_banks) + LEAD, len(hidden_order))
+            for c, b in hidden_order[first:last]:
+                if c in x_q:
+                    hidden_bank(c, b)
+
+        def relu_bank(c, b):
+            h_banks.append((c, b))
+            if b == 0:
+                h_b[c] = hq.tile([P, H_TILES, CHUNKS[c] * P], BF16, name="h_b")
+            for i in range(per_bank(c)):
+                t = b * per_bank(c) + i
+                nc.scalar.activation(
+                    out=h_b[c][:, t, :], in_=accs[(c, b)][:, i, :], func=ACT.Relu, bias=b1_f[:, t : t + 1]
                 )
 
-        def relu_group(c, t):
-            if t == 0:
-                h_b[c] = hq.tile([P, H_TILES, CHUNK], BF16, name="h_b")
-            nc.scalar.activation(out=h_b[c][:, t, :], in_=accs[(c, t)], func=ACT.Relu, bias=b1_f[:, t : t + 1])
-
         def regroup_hidden(c):
-            h_g[c] = hq.tile([P, CHUNK * PACK], BF16, name="h_g", align_bytes=64)
+            h_g[c] = hq.tile([P, CHUNKS[c] * P * PACK], BF16, name="h_g", align_bytes=64)
             nc.vector.tensor_copy(
                 out=h_g[c].rearrange("p (c i t) -> p c t i", i=4, t=PACK),
                 in_=h_b[c].rearrange("p t (c i) -> p c t i", i=4),
             )
 
         def quantise_hidden(c):
-            codes = hq.tile([P, CHUNK], U32, name="h_codes", align_bytes=64)
-            scales = hq.tile([P, CHUNK], U8, name="h_scales", align_bytes=64)
+            codes = hq.tile([P, CHUNKS[c] * P], U32, name="h_codes", align_bytes=64)
+            scales = hq.tile([P, CHUNKS[c] * P], U8, name="h_scales", align_bytes=64)
             nc.vector.quantize_mx(out=codes.bitcast(FP8X4), scales=scales, in_=h_g[c])
             h_q[c] = (codes, scales)
 
-        st_mu = {}
-        st_lv = {}
+        st = {}
 
         def stats_matmuls(c):
             codes, scales = h_q[c]
-            st_mu[c] = psum_s.tile([P, TPC, Z], F32, name="st_mu")
-            st_lv[c] = psum_s.tile([P, TPC, Z], F32, name="st_lv")
-            for j in range(TPC):
+            for j in range(CHUNKS[c]):
+                if j % 2 == 0:
+                    st[(c, j // 2)] = psum_s.tile([P, 2, 2 * Z], F32, name="st", tag=("st_0", "st_1")[j // 2])
                 tok = slice(j * P, (j + 1) * P)
-                for part, dst in enumerate((st_mu[c], st_lv[c])):
-                    cols = slice(part * Z, (part + 1) * Z)
-                    nc.tensor.matmul_mx(
-                        out=dst[:, j, :],
-                        lhsT=codes[:, tok].bitcast(FP8X4),
-                        lhsT_scale=scales[:, tok],
-                        rhs=w2_c[:, cols].bitcast(FP8X4),
-                        rhs_scale=w2_s[:, cols],
-                        start=True,
-                        stop=True,
-                    )
+                nc.tensor.matmul_mx(
+                    out=st[(c, j // 2)][:, j % 2, :],
+                    lhsT=codes[:, tok].bitcast(FP8X4),
+                    lhsT_scale=scales[:, tok],
+                    rhs=w2_c.bitcast(FP8X4),
+                    rhs_scale=w2_s,
+                    start=True,
+                    stop=True,
+                )
 
-        def chunk_tile(pool, label, dtype=F32):
-            return pool.tile([P, TPC, Z], dtype, name=label)
+        def chunk_tile(pool, c, label, dtype=F32):
+            return pool.tile([P, CHUNKS[c], Z], dtype, name=label)
 
         def store(dram, c, tile):
-            nc.sync.dma_start(out=by_tile(dram)[:, c * TPC : (c + 1) * TPC, :], in_=tile)
+            nc.sync.dma_start(out=by_tile(dram)[:, tiles_of(c), :], in_=tile)
 
-        def bias_of(part):
-            return b2_bc[:, part * Z : (part + 1) * Z].unsqueeze(1).to_broadcast([P, TPC, Z])
-
+        both = {}
         mu = {}
-        lv_raw = {}
         lv = {}
         std = {}
         inv_sd_p = {}
@@ -251,129 +277,151 @@ def tile_vrnncell_pa_t_kernel(
         sum_ex = const.tile([P, TILES], F32, name="sum_ex")
         sum_df = const.tile([P, TILES], F32, name="sum_df")
 
-        def add_bias_mean(c):
-            mu[c] = chunk_tile(outp, "mu")
-            nc.vector.tensor_tensor(out=mu[c], in0=st_mu[c], in1=bias_of(0), op=ALU.add)
+        def add_biases(c):
+            both[c] = outp.tile([P, 2, CHUNKS[c], Z], F32, name="both")
+            for b in range((CHUNKS[c] + 1) // 2):
+                tiles = slice(2 * b, min(2 * b + 2, CHUNKS[c]))
+                n = tiles.stop - tiles.start
+                nc.vector.tensor_tensor(
+                    out=both[c][:, :, tiles, :].rearrange("p a j z -> p j a z"),
+                    in0=st[(c, b)][:, 0:n, :].rearrange("p j (a z) -> p j a z", a=2),
+                    in1=b2_bc.rearrange("p (a z) -> p a z", a=2).unsqueeze(1).to_broadcast([P, n, 2, Z]),
+                    op=ALU.add,
+                )
+            mu[c] = both[c][:, 0, :, :]
             store(mu_out, c, mu[c])
 
-        def add_bias_logvar(c):
-            lv_raw[c] = chunk_tile(scr, "lv_raw")
-            nc.vector.tensor_tensor(out=lv_raw[c], in0=st_lv[c], in1=bias_of(1), op=ALU.add)
-
         def clip_logvar(c):
-            lv[c] = chunk_tile(outp, "lv")
+            lv[c] = chunk_tile(outp, c, "lv")
             nc.vector.tensor_scalar(
-                out=lv[c], in0=lv_raw[c], scalar1=-CLAMP, scalar2=CLAMP, op0=ALU.max, op1=ALU.min
+                out=lv[c], in0=both[c][:, 1, :, :], scalar1=-CLAMP, scalar2=CLAMP, op0=ALU.max, op1=ALU.min
             )
             store(lv_out, c, lv[c])
 
         def mean_difference(c):
-            diff[c] = chunk_tile(scr, "diff")
-            nc.vector.tensor_tensor(out=diff[c], in0=mu[c], in1=of_chunk(mup_sb, c), op=ALU.subtract)
+            diff[c] = chunk_tile(scr, c, "diff")
+            nc.vector.tensor_tensor(out=diff[c], in0=mu[c], in1=mup_sb[:, tiles_of(c), :], op=ALU.subtract)
 
         def scale_difference(c):
-            ratio[c] = chunk_tile(scr, "ratio")
+            ratio[c] = chunk_tile(scr, c, "ratio")
             nc.vector.tensor_tensor(out=ratio[c], in0=diff[c], in1=inv_sd_p[c], op=ALU.mult)
 
         def logvar_difference(c):
-            dlv[c] = chunk_tile(scr, "dlv")
-            for j in range(TPC):
+            dlv[c] = chunk_tile(scr, c, "dlv")
+            for j in range(CHUNKS[c]):
+                tile = FIRST[c] + j
                 nc.vector.scalar_tensor_tensor(
                     out=dlv[c][:, j, :],
                     in0=lv[c][:, j, :],
                     scalar=1.0,
-                    in1=of_chunk(lvp_sb, c)[:, j, :],
+                    in1=lvp_sb[:, tile, :],
                     op0=ALU.mult,
                     op1=ALU.subtract,
-                    accum_out=sum_df[:, c * TPC + j : c * TPC + j + 1],
+                    accum_out=sum_df[:, tile : tile + 1],
                 )
 
         def posterior_sd(c):
-            std[c] = chunk_tile(scr, "std")
+            std[c] = chunk_tile(scr, c, "std")
             nc.scalar.activation(out=std[c], in_=lv[c], func=ACT.Exp, scale=0.5)
 
         def prior_inverse_sd(c):
-            inv_sd_p[c] = chunk_tile(scr, "inv_sd_p")
-            nc.scalar.activation(out=inv_sd_p[c], in_=of_chunk(lvp_sb, c), func=ACT.Exp, scale=-0.5)
+            inv_sd_p[c] = chunk_tile(scr, c, "inv_sd_p")
+            nc.scalar.activation(out=inv_sd_p[c], in_=lvp_sb[:, tiles_of(c), :], func=ACT.Exp, scale=-0.5)
 
         def row_sums(c, func, values, sums, label):
-            unread = chunk_tile(scr, label, BF16)
-            for j in range(TPC):
+            unread = chunk_tile(scr, c, label, BF16)
+            for j in range(CHUNKS[c]):
+                tile = FIRST[c] + j
                 nc.scalar.activation(
-                    out=unread[:, j, :],
-                    in_=values[:, j, :],
-                    func=func,
-                    accum_out=sums[:, c * TPC + j : c * TPC + j + 1],
+                    out=unread[:, j, :], in_=values[:, j, :], func=func, accum_out=sums[:, tile : tile + 1]
                 )
 
         def scale_noise(c):
-            noise[c] = chunk_tile(scr, "noise")
-            nc.vector.tensor_tensor(out=noise[c], in0=std[c], in1=of_chunk(eps_sb, c), op=ALU.mult)
+            noise[c] = chunk_tile(scr, c, "noise")
+            nc.vector.tensor_tensor(out=noise[c], in0=std[c], in1=eps_sb[:, tiles_of(c), :], op=ALU.mult)
 
         def add_mean(c):
-            z = chunk_tile(outp, "z")
+            z = chunk_tile(outp, c, "z")
             nc.vector.tensor_tensor(out=z, in0=noise[c], in1=mu[c], op=ALU.add)
             store(z_out, c, z)
 
         for n in range(LEAD):
-            fill_bank(n)
-
-        w2_words = w2_sb.bitcast(F32).rearrange("p (a w u) -> p a u w", a=2, u=2)
+            fill_next()
+        copies = (nc.vector.tensor_copy, nc.scalar.copy)
+        b1_f = const.tile([P, H_TILES], F32, name="b1_f")
+        nc.vector.tensor_copy(out=b1_f, in_=b1_sb)
+        for q in range(CHUNKS[0]):
+            empty_next(copies[q % 2])
+        quantise_inputs(0)
+        w2_bank = psum_s.tile([P, 2, 2 * P], F32, name="w2_bank", tag="st_0")
+        for a in range(2):
+            for g in range(2):
+                empty_next(copies[g], refill=len(banks) < CHUNKS[0] + 4)
+            quantise_w1(a)
+            hidden_bank(0, a)
+            if a == 0:
+                transpose_words(nc, w2_bank, ident, [w2_sb.bitcast(F32)[:, w : w + WORDS] for w in (0, WORDS)])
+        for n in range(LEAD):
+            fill_next()
         w2_g = const.tile([P, 2 * Z * PACK], BF16, name="w2_g", align_bytes=64)
-        w2_bank = psum_s.tile([P, 2, 2 * P], F32, name="w2_bank", tag="st_mu")
-        transpose_words(nc, w2_bank, ident, [[w2_words[:, a, u, :] for u in range(2)] for a in range(2)])
         copy_grouped(nc.vector.tensor_copy, w2_bank, w2_g.bitcast(F32))
         w2_c = const.tile([P, 2 * Z], U32, name="w2_c", align_bytes=64)
         w2_s = const.tile([P, 2 * Z], U8, name="w2_s", align_bytes=64)
         nc.vector.quantize_mx(out=w2_c.bitcast(FP8X4), scales=w2_s, in_=w2_g)
-        b2_bank = psum_s.tile([P, 2 * Z], F32, name="b2_bank", tag="st_lv")
+        b2_bank = psum_s.tile([P, 2 * Z], F32, name="b2_bank", tag="st_1")
         nc.tensor.matmul(b2_bank, lhsT=ones, rhs=b2_row, start=True, stop=True)
         b2_bc = const.tile([P, 2 * Z], F32, name="b2_bc")
         nc.vector.tensor_copy(out=b2_bc, in_=b2_bank)
 
-        for i in range(NCH + 3):
-            if live(i - 1):
-                for t in range(H_TILES):
-                    relu_group(i - 1, t)
-                    if t + LEAD < H_TILES:
-                        hidden_group(i - 1, t + LEAD)
-            if live(i - 2):
-                add_bias_logvar(i - 2)
-                add_bias_mean(i - 2)
-                clip_logvar(i - 2)
-                mean_difference(i - 2)
-                logvar_difference(i - 2)
-                scale_difference(i - 2)
-            if live(i):
-                for q in range(4):
-                    empty_bank(4 * i + q)
-                    if 4 * i + q + LEAD < 4 * NCH:
-                        fill_bank(4 * i + q + LEAD)
-            if live(i - 1):
-                regroup_hidden(i - 1)
-            if live(i - 3):
-                scale_noise(i - 3)
-            if live(i - 1):
-                quantise_hidden(i - 1)
-                stats_matmuls(i - 1)
-            if live(i - 3):
-                add_mean(i - 3)
-            if live(i):
-                quantise_inputs(i)
-                for t in range(LEAD):
-                    hidden_group(i, t)
-            if live(i - 2):
-                posterior_sd(i - 2)
-            if live(i - 1):
-                prior_inverse_sd(i - 1)
-            if live(i - 2):
-                row_sums(i - 2, ACT.Exp, dlv[i - 2], sum_ex, "ex_unread")
-                row_sums(i - 2, ACT.Square, ratio[i - 2], sum_sq, "sq_unread")
+        def inputs(c, engines):
+            for q in range(CHUNKS[c]):
+                empty_next(engines[q % len(engines)])
 
-        total = const.tile([P, TILES], F32, name="total")
-        nc.vector.tensor_tensor(out=total, in0=sum_sq, in1=sum_ex, op=ALU.add)
-        total2 = const.tile([P, TILES], F32, name="total2")
-        nc.vector.tensor_tensor(out=total2, in0=total, in1=sum_df, op=ALU.subtract)
+        for i in range(NCH + 1):
+            if i < NCH:
+                for b in range(hidden_banks(i)):
+                    relu_bank(i, b)
+                    fill_hidden()
+            if i == 0:
+                inputs(1, copies)
+            if i >= 1:
+                add_biases(i - 1)
+                clip_logvar(i - 1)
+                mean_difference(i - 1)
+                logvar_difference(i - 1)
+                scale_difference(i - 1)
+                posterior_sd(i - 1)
+            if 1 <= i and i + 2 < NCH:
+                inputs(i + 2, (nc.scalar.copy,))
+            if i < NCH:
+                regroup_hidden(i)
+            if i == 0:
+                quantise_inputs(1)
+                fill_hidden()
+            if i >= 1:
+                scale_noise(i - 1)
+            if i < NCH:
+                quantise_hidden(i)
+                stats_matmuls(i)
+            if i == 0:
+                inputs(2, copies)
+            if i >= 1:
+                add_mean(i - 1)
+            if i + 2 < NCH:
+                quantise_inputs(i + 2)
+                fill_hidden()
+            if i >= 1:
+                row_sums(i - 1, ACT.Exp, dlv[i - 1], sum_ex, "ex_unread")
+                row_sums(i - 1, ACT.Square, ratio[i - 1], sum_sq, "sq_unread")
+            if i < NCH:
+                prior_inverse_sd(i)
+
+        linear = const.tile([P, TILES], F32, name="linear")
+        nc.vector.tensor_scalar(out=linear, in0=sum_df, scalar1=-0.5, scalar2=-0.5 * Z, op0=ALU.mult, op1=ALU.add)
+        partial = const.tile([P, TILES], F32, name="partial")
+        nc.vector.scalar_tensor_tensor(
+            out=partial, in0=sum_ex, scalar=0.5, in1=linear, op0=ALU.mult, op1=ALU.add
+        )
         kl = const.tile([P, TILES], F32, name="kl")
-        nc.vector.tensor_scalar(out=kl, in0=total2, scalar1=0.5, scalar2=-0.5 * Z, op0=ALU.mult, op1=ALU.add)
+        nc.vector.scalar_tensor_tensor(out=kl, in0=sum_sq, scalar=0.5, in1=partial, op0=ALU.mult, op1=ALU.add)
         nc.sync.dma_start(out=kl_out.rearrange("(p j) -> p j", j=TILES), in_=kl)

@@ -20,10 +20,12 @@ WORDS = K_PASS // 2
 TILES = B // P
 H_TILES = H // P
 
-CHUNKS = (2, 2, 4, 4, 4, 4, 4, 4, 2, 2)
+CHUNKS = (2, 2, 4, 4, 4, 4, 4, 4, 4)
+VECTOR_BANKS = (1, 0, 2, 1, 0, 0, 0, 0, 0)
 FIRST = tuple(sum(CHUNKS[:c]) for c in range(len(CHUNKS)))
 NCH = len(CHUNKS)
 MAX_N = max(CHUNKS)
+SHARE = 0
 LEAD = 3
 
 FLOPS = 2 * B * (O + H) * H + 2 * B * H * 2 * Z
@@ -46,7 +48,6 @@ def tile_vrnncell_pa_t_kernel(
     with ExitStack() as ctx:
         ctx.enter_context(tc.manual_schedule())
         const = ctx.enter_context(tc.tile_pool(name="const", bufs=1))
-        resident = ctx.enter_context(tc.tile_pool(name="resident", bufs=NCH))
         xq = ctx.enter_context(tc.tile_pool(name="xq", bufs=2))
         hq = ctx.enter_context(tc.tile_pool(name="hq", bufs=2))
         outp = ctx.enter_context(tc.tile_pool(name="outp", bufs=3))
@@ -68,17 +69,14 @@ def tile_vrnncell_pa_t_kernel(
         ident = const.tile([P, P], F32, name="ident")
         make_identity(nc, ident)
 
-        xh_sb = []
+        x_sb = const.tile([P, TILES * O], BF16, name="x_sb")
+        h_sb = const.tile([P, TILES * H], BF16, name="h_sb")
 
         def load_chunk(c):
-            pair = []
-            for dram, label in ((x_t, "x_in"), (h_prev, "h_in")):
-                t = resident.tile([P, CHUNKS[c] * O], BF16, name=label)
+            for dram, t in ((x_t, x_sb), (h_prev, h_sb)):
                 nc.sync.dma_start(
-                    out=t.rearrange("p (j k) -> p j k", j=CHUNKS[c]), in_=by_tile(dram)[:, tiles_of(c), :]
+                    out=t.rearrange("p (j k) -> p j k", j=TILES)[:, tiles_of(c), :], in_=by_tile(dram)[:, tiles_of(c), :]
                 )
-                pair.append(t)
-            xh_sb.append(pair)
 
         eps_sb = const.tile([P, TILES, Z], BF16, name="eps_sb")
         mup_sb = const.tile([P, TILES, Z], BF16, name="mup_sb")
@@ -89,31 +87,27 @@ def tile_vrnncell_pa_t_kernel(
             for dram, t in ((logvar_p, lvp_sb), (mu_p, mup_sb), (eps, eps_sb)):
                 nc.sync.dma_start(out=t[:, tiles, :], in_=by_tile(dram)[:, tiles, :])
 
-        load_chunk(0)
         w1_sb = const.tile([P, H_TILES * (O + H)], BF16, name="w1_sb")
-        for a in range(2):
-            rows = slice(2 * a, 2 * a + 2)
+        for t in range(H_TILES):
             nc.sync.dma_start(
-                out=w1_sb.rearrange("p (t k) -> p t k", t=H_TILES)[:, rows, :],
-                in_=enc_w1.rearrange("(p t) k -> p t k", t=H_TILES)[:, rows, :],
+                out=w1_sb.rearrange("p (t k) -> p t k", t=H_TILES)[:, t, :],
+                in_=enc_w1.rearrange("(p t) k -> p t k", t=H_TILES)[:, t, :],
             )
         b1_sb = const.tile([P, H_TILES], BF16, name="b1_sb")
         nc.scalar.dma_start(out=b1_sb, in_=enc_b1.rearrange("(p t) -> p t", t=H_TILES))
         nc.scalar.dma_start(out=b2_row[0:1, :], in_=enc_b2.rearrange("(a z) -> a z", a=1))
+        load_chunk(0)
+        load_chunk(1)
         w2_sb = const.tile([P, 2 * H], BF16, name="w2_sb")
         nc.sync.dma_start(
             out=w2_sb.rearrange("p (a k) -> p a k", a=2), in_=enc_w2.rearrange("(a p) k -> p a k", p=P)
         )
-        load_chunk(1)
-        load_prior(range(0, 2))
         load_chunk(2)
         load_chunk(3)
+        load_prior(range(0, 2))
+        load_chunk(4)
         load_prior(range(2, 5))
-        for c in range(4, 6):
-            load_chunk(c)
-        load_prior(range(5, NCH))
-        for c in range(6, NCH):
-            load_chunk(c)
+        load_chunk(5)
 
         w1_g = const.tile([P, 2 * H_TILES * P * PACK], BF16, name="w1_g", align_bytes=64)
         w1_c = const.tile([P, 2 * H_TILES * P], U32, name="w1_c", align_bytes=64)
@@ -122,26 +116,26 @@ def tile_vrnncell_pa_t_kernel(
         x_q = {}
 
         def chunk_fills(c):
-            blocks = [xh_sb[c][g].bitcast(F32)[:, j * WORDS : (j + 1) * WORDS] for g in range(2) for j in range(CHUNKS[c])]
+            tiles = range(FIRST[c], FIRST[c] + CHUNKS[c])
+            blocks = [t.bitcast(F32)[:, j * WORDS : (j + 1) * WORDS] for t in (x_sb, h_sb) for j in tiles]
             return [(blocks[2 * q : 2 * q + 2], c, q) for q in range(CHUNKS[c])]
 
         def weight_fills():
             words = w1_sb.bitcast(F32)
-            found = []
-            for a in range(2):
-                for g in range(2):
-                    starts = [((2 * a + s) * 2 + g) * WORDS for s in range(2)]
-                    found.append(([words[:, w : w + WORDS] for w in starts], None, 2 * a + g))
-            return found
+            starts = [[(2 * t + g) * WORDS for g in range(2)] for t in range(H_TILES)]
+            return [([words[:, w : w + WORDS] for w in starts[t]], None, t) for t in range(H_TILES)]
 
-        fills = chunk_fills(0) + weight_fills()
-        for c in range(1, NCH):
+        fills = weight_fills()
+        for c in range(NCH):
             fills = fills + chunk_fills(c)
         banks = []
 
         def fill_next():
             if len(banks) < len(fills):
-                bank = psum_t.tile([P, 2, 2 * P], F32, name="bank")
+                if len(banks) < LEAD:
+                    bank = psum_h.tile([P, 2, 2 * P], F32, name="bank", tag="acc")
+                else:
+                    bank = psum_t.tile([P, 2, 2 * P], F32, name="bank")
                 transpose_words(nc, bank, ident, fills[len(banks)][0])
                 banks.append(bank)
 
@@ -193,9 +187,8 @@ def tile_vrnncell_pa_t_kernel(
             tokens = CHUNKS[c] * P
             accs[(c, b)] = psum_h.tile([P, per_bank(c), tokens], F32, name="acc")
             for i in range(per_bank(c)):
-                a, s = divmod(b * per_bank(c) + i, 2)
                 for g in range(2):
-                    w_first = ((2 * a + g) * 2 + s) * P
+                    w_first = (2 * (b * per_bank(c) + i) + g) * P
                     w_cols = slice(w_first, w_first + P)
                     x_cols = slice(g * tokens, (g + 1) * tokens)
                     nc.tensor.matmul_mx(
@@ -224,15 +217,25 @@ def tile_vrnncell_pa_t_kernel(
             for i in range(per_bank(c)):
                 t = b * per_bank(c) + i
                 nc.scalar.activation(
-                    out=h_b[c][:, t, :], in_=accs[(c, b)][:, i, :], func=ACT.Relu, bias=b1_f[:, t : t + 1]
+                    out=h_b[c][:, t, :], in_=accs[(c, b)][:, i, :], func=ACT.Relu, bias=b1_sb[:, t : t + 1]
                 )
 
-        def regroup_hidden(c):
-            h_g[c] = hq.tile([P, CHUNKS[c] * P * PACK], BF16, name="h_g", align_bytes=64)
-            nc.vector.tensor_copy(
-                out=h_g[c].rearrange("p (c i t) -> p c t i", i=4, t=PACK),
-                in_=h_b[c].rearrange("p t (c i) -> p c t i", i=4),
+        def share_of(c):
+            return SHARE if CHUNKS[c] == MAX_N else 0
+
+        def regroup(copy, c, tokens):
+            copy(
+                out=h_g[c][:, tokens.start * PACK : tokens.stop * PACK].rearrange("p (c i t) -> p c t i", i=4, t=PACK),
+                in_=h_b[c][:, :, tokens].rearrange("p t (c i) -> p c t i", i=4),
             )
+
+        def regroup_share(c):
+            h_g[c] = hq.tile([P, CHUNKS[c] * P * PACK], BF16, name="h_g", align_bytes=64)
+            if share_of(c):
+                regroup(nc.scalar.copy, c, slice(CHUNKS[c] * P - share_of(c), CHUNKS[c] * P))
+
+        def regroup_hidden(c):
+            regroup(nc.vector.tensor_copy, c, slice(0, CHUNKS[c] * P - share_of(c)))
 
         def quantise_hidden(c):
             codes = hq.tile([P, CHUNKS[c] * P], U32, name="h_codes", align_bytes=64)
@@ -345,74 +348,81 @@ def tile_vrnncell_pa_t_kernel(
             nc.vector.tensor_tensor(out=z, in0=noise[c], in1=mu[c], op=ALU.add)
             store(z_out, c, z)
 
-        for n in range(LEAD):
-            fill_next()
         copies = (nc.vector.tensor_copy, nc.scalar.copy)
-        b1_f = const.tile([P, H_TILES], F32, name="b1_f")
-        nc.vector.tensor_copy(out=b1_f, in_=b1_sb)
-        for q in range(CHUNKS[0]):
-            empty_next(copies[q % 2])
-        quantise_inputs(0)
-        w2_bank = psum_s.tile([P, 2, 2 * P], F32, name="w2_bank", tag="st_0")
-        for a in range(2):
-            for g in range(2):
-                empty_next(copies[g], refill=len(banks) < CHUNKS[0] + 4)
-            quantise_w1(a)
-            hidden_bank(0, a)
-            if a == 0:
-                transpose_words(nc, w2_bank, ident, [w2_sb.bitcast(F32)[:, w : w + WORDS] for w in (0, WORDS)])
-        for n in range(LEAD):
+
+        def inputs(c, banks_of_chunk):
+            for q in banks_of_chunk:
+                empty_next(nc.vector.tensor_copy if q < VECTOR_BANKS[c] else nc.scalar.copy)
+
+        for n in range(H_TILES + CHUNKS[0]):
             fill_next()
+        b2_bank = psum_s.tile([P, 2 * Z], F32, name="b2_bank", tag="st_1")
+        nc.tensor.matmul(b2_bank, lhsT=ones, rhs=b2_row, start=True, stop=True)
+        for n in range(3):
+            empty_next(copies[n % 2], refill=False)
+        quantise_w1(0)
+        empty_next(nc.scalar.copy)
+        empty_next(nc.vector.tensor_copy)
+        empty_next(nc.scalar.copy)
+        quantise_w1(1)
+        quantise_inputs(0)
+        fill_hidden()
+        w2_bank = psum_s.tile([P, 2, 2 * P], F32, name="w2_bank", tag="st_0")
+        transpose_words(nc, w2_bank, ident, [w2_sb.bitcast(F32)[:, w : w + WORDS] for w in (0, WORDS)])
+        inputs(1, range(CHUNKS[1]))
+        quantise_inputs(1)
+        b2_bc = const.tile([P, 2 * Z], F32, name="b2_bc")
+        nc.scalar.copy(out=b2_bc, in_=b2_bank)
         w2_g = const.tile([P, 2 * Z * PACK], BF16, name="w2_g", align_bytes=64)
         copy_grouped(nc.vector.tensor_copy, w2_bank, w2_g.bitcast(F32))
         w2_c = const.tile([P, 2 * Z], U32, name="w2_c", align_bytes=64)
         w2_s = const.tile([P, 2 * Z], U8, name="w2_s", align_bytes=64)
-        nc.vector.quantize_mx(out=w2_c.bitcast(FP8X4), scales=w2_s, in_=w2_g)
-        b2_bank = psum_s.tile([P, 2 * Z], F32, name="b2_bank", tag="st_1")
-        nc.tensor.matmul(b2_bank, lhsT=ones, rhs=b2_row, start=True, stop=True)
-        b2_bc = const.tile([P, 2 * Z], F32, name="b2_bc")
-        nc.vector.tensor_copy(out=b2_bc, in_=b2_bank)
 
-        def inputs(c, engines):
-            for q in range(CHUNKS[c]):
-                empty_next(engines[q % len(engines)])
-
-        for i in range(NCH + 1):
+        for i in range(NCH + 2):
+            last = CHUNKS[i + 2] - 1 if i + 2 < NCH else 0
+            if i >= 1 and i + 5 < NCH:
+                load_chunk(i + 5)
+                load_prior(range(i + 4, i + 5))
+            elif i + 4 < NCH and i >= 1:
+                load_prior(range(i + 4, i + 5))
             if i < NCH:
                 for b in range(hidden_banks(i)):
                     relu_bank(i, b)
-                    fill_hidden()
-            if i == 0:
-                inputs(1, copies)
-            if i >= 1:
+                    if i > 0:
+                        fill_hidden()
+                regroup_share(i)
+            if 1 <= i <= NCH:
                 add_biases(i - 1)
+            if i >= 2:
+                add_mean(i - 2)
+            if 1 <= i <= NCH:
                 clip_logvar(i - 1)
                 mean_difference(i - 1)
-                logvar_difference(i - 1)
-                scale_difference(i - 1)
                 posterior_sd(i - 1)
-            if 1 <= i and i + 2 < NCH:
-                inputs(i + 2, (nc.scalar.copy,))
+            if i + 2 < NCH:
+                inputs(i + 2, range(0, last))
             if i < NCH:
                 regroup_hidden(i)
             if i == 0:
-                quantise_inputs(1)
+                nc.vector.quantize_mx(out=w2_c.bitcast(FP8X4), scales=w2_s, in_=w2_g)
+            if 1 <= i <= NCH:
+                logvar_difference(i - 1)
+            if i == 0:
                 fill_hidden()
-            if i >= 1:
-                scale_noise(i - 1)
             if i < NCH:
                 quantise_hidden(i)
                 stats_matmuls(i)
-            if i == 0:
-                inputs(2, copies)
-            if i >= 1:
-                add_mean(i - 1)
+            if i + 2 < NCH:
+                inputs(i + 2, range(last, last + 1))
+            if 1 <= i <= NCH:
+                scale_difference(i - 1)
+                scale_noise(i - 1)
             if i + 2 < NCH:
                 quantise_inputs(i + 2)
                 fill_hidden()
-            if i >= 1:
-                row_sums(i - 1, ACT.Exp, dlv[i - 1], sum_ex, "ex_unread")
-                row_sums(i - 1, ACT.Square, ratio[i - 1], sum_sq, "sq_unread")
+            if i >= 2:
+                row_sums(i - 2, ACT.Exp, dlv[i - 2], sum_ex, "ex_unread")
+                row_sums(i - 2, ACT.Square, ratio[i - 2], sum_sq, "sq_unread")
             if i < NCH:
                 prior_inverse_sd(i)
 

@@ -21,11 +21,10 @@ TILES = B // P
 H_TILES = H // P
 
 CHUNKS = (2, 2, 4, 4, 4, 4, 4, 4, 4)
-VECTOR_BANKS = (1, 0, 2, 1, 0, 0, 0, 0, 0)
 FIRST = tuple(sum(CHUNKS[:c]) for c in range(len(CHUNKS)))
 NCH = len(CHUNKS)
 MAX_N = max(CHUNKS)
-SHARE = 0
+SQV = 1
 LEAD = 3
 
 FLOPS = 2 * B * (O + H) * H + 2 * B * H * 2 * Z
@@ -220,22 +219,22 @@ def tile_vrnncell_pa_t_kernel(
                     out=h_b[c][:, t, :], in_=accs[(c, b)][:, i, :], func=ACT.Relu, bias=b1_sb[:, t : t + 1]
                 )
 
-        def share_of(c):
-            return SHARE if CHUNKS[c] == MAX_N else 0
-
-        def regroup(copy, c, tokens):
+        def regroup(copy, c, tiles):
+            first, stop = tiles.start * P, tiles.stop * P
             copy(
-                out=h_g[c][:, tokens.start * PACK : tokens.stop * PACK].rearrange("p (c i t) -> p c t i", i=4, t=PACK),
-                in_=h_b[c][:, :, tokens].rearrange("p t (c i) -> p c t i", i=4),
+                out=h_g[c][:, first * PACK : stop * PACK].rearrange("p (c i t) -> p c t i", i=4, t=PACK),
+                in_=h_b[c][:, :, first:stop].rearrange("p t (c i) -> p c t i", i=4),
             )
 
-        def regroup_share(c):
-            h_g[c] = hq.tile([P, CHUNKS[c] * P * PACK], BF16, name="h_g", align_bytes=64)
-            if share_of(c):
-                regroup(nc.scalar.copy, c, slice(CHUNKS[c] * P - share_of(c), CHUNKS[c] * P))
+        def scalar_regroups(c):
+            return CHUNKS[c] // 2 if c >= NCH - 2 else 0
 
         def regroup_hidden(c):
-            regroup(nc.vector.tensor_copy, c, slice(0, CHUNKS[c] * P - share_of(c)))
+            h_g[c] = hq.tile([P, CHUNKS[c] * P * PACK], BF16, name="h_g", align_bytes=64)
+            split = CHUNKS[c] - scalar_regroups(c)
+            regroup(nc.vector.tensor_copy, c, range(split))
+            if split < CHUNKS[c]:
+                regroup(nc.scalar.copy, c, range(split, CHUNKS[c]))
 
         def quantise_hidden(c):
             codes = hq.tile([P, CHUNKS[c] * P], U32, name="h_codes", align_bytes=64)
@@ -331,12 +330,35 @@ def tile_vrnncell_pa_t_kernel(
             inv_sd_p[c] = chunk_tile(scr, c, "inv_sd_p")
             nc.scalar.activation(out=inv_sd_p[c], in_=lvp_sb[:, tiles_of(c), :], func=ACT.Exp, scale=-0.5)
 
-        def row_sums(c, func, values, sums, label):
+        def row_sums(c, func, values, sums, label, tiles):
             unread = chunk_tile(scr, c, label, BF16)
-            for j in range(CHUNKS[c]):
+            for j in tiles:
                 tile = FIRST[c] + j
                 nc.scalar.activation(
                     out=unread[:, j, :], in_=values[:, j, :], func=func, accum_out=sums[:, tile : tile + 1]
+                )
+
+        def vector_squares(c):
+            return 2 if c == NCH - 1 else SQV
+
+        def sum_exponentials(c):
+            row_sums(c, ACT.Exp, dlv[c], sum_ex, "ex_unread", range(CHUNKS[c]))
+
+        def sum_squares(c):
+            row_sums(c, ACT.Square, ratio[c], sum_sq, "sq_unread", range(vector_squares(c), CHUNKS[c]))
+
+        def sum_squares_vector(c):
+            unread = chunk_tile(scr, c, "sv_unread")
+            for j in range(vector_squares(c)):
+                tile = FIRST[c] + j
+                nc.vector.scalar_tensor_tensor(
+                    out=unread[:, j, :],
+                    in0=ratio[c][:, j, :],
+                    scalar=1.0,
+                    in1=ratio[c][:, j, :],
+                    op0=ALU.mult,
+                    op1=ALU.mult,
+                    accum_out=sum_sq[:, tile : tile + 1],
                 )
 
         def scale_noise(c):
@@ -345,14 +367,15 @@ def tile_vrnncell_pa_t_kernel(
 
         def add_mean(c):
             z = chunk_tile(outp, c, "z")
-            nc.vector.tensor_tensor(out=z, in0=noise[c], in1=mu[c], op=ALU.add)
+            engine = nc.vector if c == NCH - 1 else nc.gpsimd
+            engine.tensor_tensor(out=z, in0=noise[c], in1=mu[c], op=ALU.add)
             store(z_out, c, z)
 
         copies = (nc.vector.tensor_copy, nc.scalar.copy)
 
         def inputs(c, banks_of_chunk):
             for q in banks_of_chunk:
-                empty_next(nc.vector.tensor_copy if q < VECTOR_BANKS[c] else nc.scalar.copy)
+                empty_next(nc.scalar.copy)
 
         for n in range(H_TILES + CHUNKS[0]):
             fill_next()
@@ -363,12 +386,13 @@ def tile_vrnncell_pa_t_kernel(
         quantise_w1(0)
         empty_next(nc.scalar.copy)
         empty_next(nc.vector.tensor_copy)
-        empty_next(nc.scalar.copy)
+        empty_next(nc.scalar.copy, refill=False)
         quantise_w1(1)
         quantise_inputs(0)
         fill_hidden()
         w2_bank = psum_s.tile([P, 2, 2 * P], F32, name="w2_bank", tag="st_0")
         transpose_words(nc, w2_bank, ident, [w2_sb.bitcast(F32)[:, w : w + WORDS] for w in (0, WORDS)])
+        fill_next()
         inputs(1, range(CHUNKS[1]))
         quantise_inputs(1)
         b2_bc = const.tile([P, 2 * Z], F32, name="b2_bc")
@@ -378,7 +402,7 @@ def tile_vrnncell_pa_t_kernel(
         w2_c = const.tile([P, 2 * Z], U32, name="w2_c", align_bytes=64)
         w2_s = const.tile([P, 2 * Z], U8, name="w2_s", align_bytes=64)
 
-        for i in range(NCH + 2):
+        for i in range(NCH + 1):
             last = CHUNKS[i + 2] - 1 if i + 2 < NCH else 0
             if i >= 1 and i + 5 < NCH:
                 load_chunk(i + 5)
@@ -390,22 +414,24 @@ def tile_vrnncell_pa_t_kernel(
                     relu_bank(i, b)
                     if i > 0:
                         fill_hidden()
-                regroup_share(i)
-            if 1 <= i <= NCH:
+            if i >= 1:
                 add_biases(i - 1)
-            if i >= 2:
-                add_mean(i - 2)
-            if 1 <= i <= NCH:
+            if 2 <= i < NCH:
+                scale_difference(i - 2)
+            if i >= 1:
                 clip_logvar(i - 1)
-                mean_difference(i - 1)
                 posterior_sd(i - 1)
+            if i >= 2:
+                sum_squares_vector(i - 2)
+            if i >= 1:
+                mean_difference(i - 1)
             if i + 2 < NCH:
                 inputs(i + 2, range(0, last))
             if i < NCH:
                 regroup_hidden(i)
             if i == 0:
                 nc.vector.quantize_mx(out=w2_c.bitcast(FP8X4), scales=w2_s, in_=w2_g)
-            if 1 <= i <= NCH:
+            if i >= 1:
                 logvar_difference(i - 1)
             if i == 0:
                 fill_hidden()
@@ -414,15 +440,23 @@ def tile_vrnncell_pa_t_kernel(
                 stats_matmuls(i)
             if i + 2 < NCH:
                 inputs(i + 2, range(last, last + 1))
-            if 1 <= i <= NCH:
-                scale_difference(i - 1)
+            if i >= 1:
                 scale_noise(i - 1)
+            if i >= NCH - 1:
+                scale_difference(i - 1)
             if i + 2 < NCH:
                 quantise_inputs(i + 2)
                 fill_hidden()
-            if i >= 2:
-                row_sums(i - 2, ACT.Exp, dlv[i - 2], sum_ex, "ex_unread")
-                row_sums(i - 2, ACT.Square, ratio[i - 2], sum_sq, "sq_unread")
+            if i >= 1:
+                add_mean(i - 1)
+            if i == NCH:
+                sum_squares_vector(i - 1)
+            if 2 <= i < NCH:
+                sum_exponentials(i - 2)
+                sum_squares(i - 2)
+            if i >= NCH - 1:
+                sum_exponentials(i - 1)
+                sum_squares(i - 1)
             if i < NCH:
                 prior_inverse_sd(i)
 

@@ -24,7 +24,6 @@ CHUNKS = (2, 2, 4, 4, 4, 4, 4, 4, 4)
 FIRST = tuple(sum(CHUNKS[:c]) for c in range(len(CHUNKS)))
 NCH = len(CHUNKS)
 MAX_N = max(CHUNKS)
-SQV = 1
 LEAD = 3
 
 FLOPS = 2 * B * (O + H) * H + 2 * B * H * 2 * Z
@@ -339,7 +338,7 @@ def tile_vrnncell_pa_t_kernel(
                 )
 
         def vector_squares(c):
-            return 2 if c == NCH - 1 else SQV
+            return CHUNKS[c] // 2 if c == NCH - 1 else 0
 
         def sum_exponentials(c):
             row_sums(c, ACT.Exp, dlv[c], sum_ex, "ex_unread", range(CHUNKS[c]))
@@ -365,17 +364,31 @@ def tile_vrnncell_pa_t_kernel(
             noise[c] = chunk_tile(scr, c, "noise")
             nc.vector.tensor_tensor(out=noise[c], in0=std[c], in1=eps_sb[:, tiles_of(c), :], op=ALU.mult)
 
-        def add_mean(c):
-            z = chunk_tile(outp, c, "z")
-            engine = nc.vector if c == NCH - 1 else nc.gpsimd
-            engine.tensor_tensor(out=z, in0=noise[c], in1=mu[c], op=ALU.add)
-            store(z_out, c, z)
+        z = {}
+
+        def gpsimd_adds(c):
+            return 0 if c == NCH - 1 else CHUNKS[c] * 3 // 4
+
+        def add_mean_part(engine, c, first, stop):
+            engine.tensor_tensor(
+                out=z[c][:, first:stop, :], in0=noise[c][:, first:stop, :], in1=mu[c][:, first:stop, :], op=ALU.add
+            )
+
+        def add_mean_gpsimd(c):
+            z[c] = chunk_tile(outp, c, "z")
+            if gpsimd_adds(c):
+                add_mean_part(nc.gpsimd, c, 0, gpsimd_adds(c))
+
+        def add_mean_vector(c):
+            if gpsimd_adds(c) < CHUNKS[c]:
+                add_mean_part(nc.vector, c, gpsimd_adds(c), CHUNKS[c])
+            store(z_out, c, z[c])
 
         copies = (nc.vector.tensor_copy, nc.scalar.copy)
 
-        def inputs(c, banks_of_chunk):
+        def inputs(c, banks_of_chunk, refill=True):
             for q in banks_of_chunk:
-                empty_next(nc.scalar.copy)
+                empty_next(nc.scalar.copy, refill)
 
         for n in range(H_TILES + CHUNKS[0]):
             fill_next()
@@ -420,24 +433,29 @@ def tile_vrnncell_pa_t_kernel(
                 scale_difference(i - 2)
             if i >= 1:
                 clip_logvar(i - 1)
-                posterior_sd(i - 1)
             if i >= 2:
-                sum_squares_vector(i - 2)
+                add_mean_vector(i - 2)
             if i >= 1:
                 mean_difference(i - 1)
             if i + 2 < NCH:
-                inputs(i + 2, range(0, last))
+                inputs(i + 2, range(0, 1))
+                inputs(i + 2, range(1, last), refill=i > 1)
+            if i >= 1:
+                posterior_sd(i - 1)
             if i < NCH:
                 regroup_hidden(i)
             if i == 0:
                 nc.vector.quantize_mx(out=w2_c.bitcast(FP8X4), scales=w2_s, in_=w2_g)
             if i >= 1:
                 logvar_difference(i - 1)
-            if i == 0:
-                fill_hidden()
             if i < NCH:
                 quantise_hidden(i)
                 stats_matmuls(i)
+            if i == 0:
+                fill_hidden()
+            if i <= 1:
+                for n in range(LEAD - 1):
+                    fill_next()
             if i + 2 < NCH:
                 inputs(i + 2, range(last, last + 1))
             if i >= 1:
@@ -448,7 +466,9 @@ def tile_vrnncell_pa_t_kernel(
                 quantise_inputs(i + 2)
                 fill_hidden()
             if i >= 1:
-                add_mean(i - 1)
+                add_mean_gpsimd(i - 1)
+            if i == NCH:
+                add_mean_vector(i - 1)
             if i == NCH:
                 sum_squares_vector(i - 1)
             if 2 <= i < NCH:

@@ -70,8 +70,9 @@ def tile_vrnncell_pa_t_kernel(
         x_sb = const.tile([P, TILES * O], BF16, name="x_sb")
         h_sb = const.tile([P, TILES * H], BF16, name="h_sb")
 
-        def load_chunk(c):
-            for dram, t in ((x_t, x_sb), (h_prev, h_sb)):
+        def load_chunk(c, parts=(0, 1)):
+            for part in parts:
+                dram, t = ((x_t, x_sb), (h_prev, h_sb))[part]
                 nc.sync.dma_start(
                     out=t.rearrange("p (j k) -> p j k", j=TILES)[:, tiles_of(c), :], in_=by_tile(dram)[:, tiles_of(c), :]
                 )
@@ -96,11 +97,12 @@ def tile_vrnncell_pa_t_kernel(
         nc.scalar.dma_start(out=b2_row[0:1, :], in_=enc_b2.rearrange("(a z) -> a z", a=1))
         load_chunk(0)
         load_chunk(1)
+        load_chunk(2, (0,))
         w2_sb = const.tile([P, 2 * H], BF16, name="w2_sb")
         nc.sync.dma_start(
             out=w2_sb.rearrange("p (a k) -> p a k", a=2), in_=enc_w2.rearrange("(a p) k -> p a k", p=P)
         )
-        load_chunk(2)
+        load_chunk(2, (1,))
         load_chunk(3)
         load_prior(range(0, 2))
         load_chunk(4)
@@ -329,36 +331,19 @@ def tile_vrnncell_pa_t_kernel(
             inv_sd_p[c] = chunk_tile(scr, c, "inv_sd_p")
             nc.scalar.activation(out=inv_sd_p[c], in_=lvp_sb[:, tiles_of(c), :], func=ACT.Exp, scale=-0.5)
 
-        def row_sums(c, func, values, sums, label, tiles):
+        def row_sums(c, func, values, sums, label):
             unread = chunk_tile(scr, c, label, BF16)
-            for j in tiles:
+            for j in range(CHUNKS[c]):
                 tile = FIRST[c] + j
                 nc.scalar.activation(
                     out=unread[:, j, :], in_=values[:, j, :], func=func, accum_out=sums[:, tile : tile + 1]
                 )
 
-        def vector_squares(c):
-            return CHUNKS[c] // 2 if c == NCH - 1 else 0
-
         def sum_exponentials(c):
-            row_sums(c, ACT.Exp, dlv[c], sum_ex, "ex_unread", range(CHUNKS[c]))
+            row_sums(c, ACT.Exp, dlv[c], sum_ex, "ex_unread")
 
         def sum_squares(c):
-            row_sums(c, ACT.Square, ratio[c], sum_sq, "sq_unread", range(vector_squares(c), CHUNKS[c]))
-
-        def sum_squares_vector(c):
-            unread = chunk_tile(scr, c, "sv_unread")
-            for j in range(vector_squares(c)):
-                tile = FIRST[c] + j
-                nc.vector.scalar_tensor_tensor(
-                    out=unread[:, j, :],
-                    in0=ratio[c][:, j, :],
-                    scalar=1.0,
-                    in1=ratio[c][:, j, :],
-                    op0=ALU.mult,
-                    op1=ALU.mult,
-                    accum_out=sum_sq[:, tile : tile + 1],
-                )
+            row_sums(c, ACT.Square, ratio[c], sum_sq, "sq_unread")
 
         def scale_noise(c):
             noise[c] = chunk_tile(scr, c, "noise")
@@ -386,6 +371,10 @@ def tile_vrnncell_pa_t_kernel(
 
         copies = (nc.vector.tensor_copy, nc.scalar.copy)
 
+        def fill_banks():
+            while len(banks) - len(emptied) < LEAD and len(banks) < len(fills):
+                fill_next()
+
         def inputs(c, banks_of_chunk, refill=True):
             for q in banks_of_chunk:
                 empty_next(nc.scalar.copy, refill)
@@ -399,19 +388,19 @@ def tile_vrnncell_pa_t_kernel(
         quantise_w1(0)
         empty_next(nc.scalar.copy)
         empty_next(nc.vector.tensor_copy)
-        empty_next(nc.scalar.copy, refill=False)
+        empty_next(nc.scalar.copy)
         quantise_w1(1)
         quantise_inputs(0)
         fill_hidden()
+        empty_next(nc.scalar.copy)
         w2_bank = psum_s.tile([P, 2, 2 * P], F32, name="w2_bank", tag="st_0")
         transpose_words(nc, w2_bank, ident, [w2_sb.bitcast(F32)[:, w : w + WORDS] for w in (0, WORDS)])
-        fill_next()
-        inputs(1, range(CHUNKS[1]))
+        empty_next(nc.scalar.copy)
         quantise_inputs(1)
         b2_bc = const.tile([P, 2 * Z], F32, name="b2_bc")
         nc.scalar.copy(out=b2_bc, in_=b2_bank)
+        empty_next(nc.scalar.copy)
         w2_g = const.tile([P, 2 * Z * PACK], BF16, name="w2_g", align_bytes=64)
-        copy_grouped(nc.vector.tensor_copy, w2_bank, w2_g.bitcast(F32))
         w2_c = const.tile([P, 2 * Z], U32, name="w2_c", align_bytes=64)
         w2_s = const.tile([P, 2 * Z], U8, name="w2_s", align_bytes=64)
 
@@ -425,8 +414,10 @@ def tile_vrnncell_pa_t_kernel(
             if i < NCH:
                 for b in range(hidden_banks(i)):
                     relu_bank(i, b)
-                    if i > 0:
-                        fill_hidden()
+                    if i >= 1 and b == 0:
+                        if i >= 2:
+                            fill_hidden()
+                        fill_banks()
             if i >= 1:
                 add_biases(i - 1)
             if 2 <= i < NCH:
@@ -438,39 +429,44 @@ def tile_vrnncell_pa_t_kernel(
             if i >= 1:
                 mean_difference(i - 1)
             if i + 2 < NCH:
-                inputs(i + 2, range(0, 1))
-                inputs(i + 2, range(1, last), refill=i > 1)
+                if i > 0:
+                    inputs(i + 2, range(0, 1))
+                if i > 0:
+                    fill_hidden()
+                inputs(i + 2, range(1, last), refill=False)
+            if i >= 1:
+                fill_hidden()
             if i >= 1:
                 posterior_sd(i - 1)
             if i < NCH:
                 regroup_hidden(i)
             if i == 0:
+                copy_grouped(nc.vector.tensor_copy, w2_bank, w2_g.bitcast(F32))
+                quantise_hidden(0)
                 nc.vector.quantize_mx(out=w2_c.bitcast(FP8X4), scales=w2_s, in_=w2_g)
             if i >= 1:
                 logvar_difference(i - 1)
-            if i < NCH:
+            if 1 <= i < NCH:
                 quantise_hidden(i)
-                stats_matmuls(i)
             if i == 0:
                 fill_hidden()
-            if i <= 1:
+            if i < NCH:
+                stats_matmuls(i)
+            if i == 0:
                 for n in range(LEAD - 1):
                     fill_next()
             if i + 2 < NCH:
-                inputs(i + 2, range(last, last + 1))
+                inputs(i + 2, range(last, last + 1), refill=False)
             if i >= 1:
                 scale_noise(i - 1)
             if i >= NCH - 1:
                 scale_difference(i - 1)
             if i + 2 < NCH:
                 quantise_inputs(i + 2)
-                fill_hidden()
             if i >= 1:
                 add_mean_gpsimd(i - 1)
             if i == NCH:
                 add_mean_vector(i - 1)
-            if i == NCH:
-                sum_squares_vector(i - 1)
             if 2 <= i < NCH:
                 sum_exponentials(i - 2)
                 sum_squares(i - 2)

from contextlib import ExitStack

import concourse.mybir as mybir
from concourse.masks import make_identity

F32 = mybir.dt.float32
BF16 = mybir.dt.bfloat16
U32 = mybir.dt.uint32
U8 = mybir.dt.uint8
FP8X4 = mybir.dt.float8_e4m3fn_x4
ACT = mybir.ActivationFunctionType
ALU = mybir.AluOpType

P = 128
B, O, H, Z = 4096, 512, 512, 128
CLAMP = 10.0
PACK = 4
K_PASS = P * PACK
WORDS = K_PASS // 2
TILES = B // P
H_TILES = H // P

CHUNKS = (2, 2, 4, 4, 4, 4, 4, 4, 4)
FIRST = tuple(sum(CHUNKS[:c]) for c in range(len(CHUNKS)))
NCH = len(CHUNKS)
MAX_N = max(CHUNKS)
LEAD = 3

FLOPS = 2 * B * (O + H) * H + 2 * B * H * 2 * Z


def transpose_words(nc, bank, ident, blocks):
    for s, words in enumerate(blocks):
        for u in range(2):
            nc.tensor.transpose(bank[:, u, s * P : (s + 1) * P], words[:, u:WORDS:2], ident)


def copy_grouped(copy, bank, grouped_words):
    copy(out=grouped_words.rearrange("p (c u) -> p c u", u=2), in_=bank.rearrange("p u c -> p c u"))


def tile_vrnncell_pa_t_kernel(
    tc, x_t, h_prev, eps, enc_w1, enc_b1, enc_w2, enc_b2, mu_p, logvar_p, z_out, mu_out, lv_out, kl_out
):
    nc = tc.nc
    with ExitStack() as ctx:
        ctx.enter_context(tc.manual_schedule())
        const = ctx.enter_context(tc.tile_pool(name="const", bufs=1))
        xq = ctx.enter_context(tc.tile_pool(name="xq", bufs=2))
        hq = ctx.enter_context(tc.tile_pool(name="hq", bufs=2))
        outp = ctx.enter_context(tc.tile_pool(name="outp", bufs=3))
        scr = ctx.enter_context(tc.tile_pool(name="scr", bufs=2))
        psum_t = ctx.enter_context(tc.psum_pool(name="psum_t", bufs=LEAD))
        psum_h = ctx.enter_context(tc.psum_pool(name="psum_h", bufs=LEAD))
        psum_s = ctx.enter_context(tc.psum_pool(name="psum_s", bufs=1))

        def by_tile(dram):
            return dram.rearrange("(p j) z -> p j z", j=TILES)

        def tiles_of(c):
            return slice(FIRST[c], FIRST[c] + CHUNKS[c])

        b2_row = const.tile([P, 2 * Z], BF16, name="b2_row")
        nc.gpsimd.memset(b2_row, 0.0)
        ones = const.tile([P, P], BF16, name="ones")
        nc.gpsimd.memset(ones, 1.0)
        ident = const.tile([P, P], F32, name="ident")
        make_identity(nc, ident)

        x_sb = const.tile([P, TILES * O], BF16, name="x_sb")
        h_sb = const.tile([P, TILES * H], BF16, name="h_sb")

        def load_chunk(c, parts=(0, 1)):
            for part in parts:
                dram, t = ((x_t, x_sb), (h_prev, h_sb))[part]
                nc.sync.dma_start(
                    out=t.rearrange("p (j k) -> p j k", j=TILES)[:, tiles_of(c), :], in_=by_tile(dram)[:, tiles_of(c), :]
                )

        eps_sb = const.tile([P, TILES, Z], BF16, name="eps_sb")
        mup_sb = const.tile([P, TILES, Z], BF16, name="mup_sb")
        lvp_sb = const.tile([P, TILES, Z], BF16, name="lvp_sb")

        def load_prior(chunks):
            tiles = slice(tiles_of(chunks[0]).start, tiles_of(chunks[-1]).stop)
            for dram, t in ((logvar_p, lvp_sb), (mu_p, mup_sb), (eps, eps_sb)):
                nc.sync.dma_start(out=t[:, tiles, :], in_=by_tile(dram)[:, tiles, :])

        w1_sb = const.tile([P, H_TILES * (O + H)], BF16, name="w1_sb")
        for t in range(H_TILES):
            nc.sync.dma_start(
                out=w1_sb.rearrange("p (t k) -> p t k", t=H_TILES)[:, t, :],
                in_=enc_w1.rearrange("(p t) k -> p t k", t=H_TILES)[:, t, :],
            )
        b1_sb = const.tile([P, H_TILES], BF16, name="b1_sb")
        nc.scalar.dma_start(out=b1_sb, in_=enc_b1.rearrange("(p t) -> p t", t=H_TILES))
        nc.scalar.dma_start(out=b2_row[0:1, :], in_=enc_b2.rearrange("(a z) -> a z", a=1))
        load_chunk(0)
        load_chunk(1)
        load_chunk(2, (0,))
        w2_sb = const.tile([P, 2 * H], BF16, name="w2_sb")
        nc.sync.dma_start(
            out=w2_sb.rearrange("p (a k) -> p a k", a=2), in_=enc_w2.rearrange("(a p) k -> p a k", p=P)
        )
        load_chunk(2, (1,))
        load_chunk(3)
        load_prior(range(0, 2))
        load_chunk(4)
        load_prior(range(2, 5))
        load_chunk(5)

        w1_g = const.tile([P, 2 * H_TILES * P * PACK], BF16, name="w1_g", align_bytes=64)
        w1_c = const.tile([P, 2 * H_TILES * P], U32, name="w1_c", align_bytes=64)
        w1_s = const.tile([P, 2 * H_TILES * P], U8, name="w1_s", align_bytes=64)
        x_g = {}
        x_q = {}

        def chunk_fills(c):
            tiles = range(FIRST[c], FIRST[c] + CHUNKS[c])
            blocks = [t.bitcast(F32)[:, j * WORDS : (j + 1) * WORDS] for t in (x_sb, h_sb) for j in tiles]
            return [(blocks[2 * q : 2 * q + 2], c, q) for q in range(CHUNKS[c])]

        def weight_fills():
            words = w1_sb.bitcast(F32)
            starts = [[(2 * t + g) * WORDS for g in range(2)] for t in range(H_TILES)]
            return [([words[:, w : w + WORDS] for w in starts[t]], None, t) for t in range(H_TILES)]

        fills = weight_fills()
        for c in range(NCH):
            fills = fills + chunk_fills(c)
        banks = []

        def fill_next():
            if len(banks) < len(fills):
                if len(banks) < LEAD:
                    bank = psum_h.tile([P, 2, 2 * P], F32, name="bank", tag="acc")
                else:
                    bank = psum_t.tile([P, 2, 2 * P], F32, name="bank")
                transpose_words(nc, bank, ident, fills[len(banks)][0])
                banks.append(bank)

        emptied = []

        def empty_next(copy, refill=True):
            n = len(emptied)
            c, q = fills[n][1:]
            if c is None:
                grouped = w1_g
            else:
                if q == 0:
                    x_g[c] = xq.tile([P, 2 * CHUNKS[c] * P * PACK], BF16, name="x_g", align_bytes=64)
                grouped = x_g[c]
            copy_grouped(copy, banks[n], grouped.bitcast(F32)[:, q * 4 * P : (q + 1) * 4 * P])
            emptied.append(n)
            if refill:
                fill_next()

        def quantise_w1(a):
            cols = slice(a * 4 * P, (a + 1) * 4 * P)
            nc.vector.quantize_mx(
                out=w1_c[:, cols].bitcast(FP8X4),
                scales=w1_s[:, cols],
                in_=w1_g[:, a * 4 * P * PACK : (a + 1) * 4 * P * PACK],
            )

        def quantise_inputs(c):
            width = 2 * CHUNKS[c] * P
            codes = xq.tile([P, width], U32, name="x_codes", align_bytes=64)
            scales = xq.tile([P, width], U8, name="x_scales", align_bytes=64)
            nc.vector.quantize_mx(out=codes.bitcast(FP8X4), scales=scales, in_=x_g[c])
            x_q[c] = (codes, scales)

        accs = {}
        h_banks = []
        h_b = {}
        h_g = {}
        h_q = {}

        def per_bank(c):
            return MAX_N // CHUNKS[c]

        def hidden_banks(c):
            return H_TILES // per_bank(c)

        def hidden_bank(c, b):
            codes, scales = x_q[c]
            tokens = CHUNKS[c] * P
            accs[(c, b)] = psum_h.tile([P, per_bank(c), tokens], F32, name="acc")
            for i in range(per_bank(c)):
                for g in range(2):
                    w_first = (2 * (b * per_bank(c) + i) + g) * P
                    w_cols = slice(w_first, w_first + P)
                    x_cols = slice(g * tokens, (g + 1) * tokens)
                    nc.tensor.matmul_mx(
                        out=accs[(c, b)][:, i, :],
                        lhsT=w1_c[:, w_cols].bitcast(FP8X4),
                        lhsT_scale=w1_s[:, w_cols],
                        rhs=codes[:, x_cols].bitcast(FP8X4),
                        rhs_scale=scales[:, x_cols],
                        start=(g == 0),
                        stop=(g == 1),
                    )

        hidden_order = [(c, b) for c in range(NCH) for b in range(hidden_banks(c))]

        def fill_hidden():
            first = len(accs)
            last = min(len(h_banks) + LEAD, len(hidden_order))
            for c, b in hidden_order[first:last]:
                if c in x_q:
                    hidden_bank(c, b)

        def relu_bank(c, b):
            h_banks.append((c, b))
            if b == 0:
                h_b[c] = hq.tile([P, H_TILES, CHUNKS[c] * P], BF16, name="h_b")
            for i in range(per_bank(c)):
                t = b * per_bank(c) + i
                nc.scalar.activation(
                    out=h_b[c][:, t, :], in_=accs[(c, b)][:, i, :], func=ACT.Relu, bias=b1_sb[:, t : t + 1]
                )

        def regroup(copy, c, tiles):
            first, stop = tiles.start * P, tiles.stop * P
            copy(
                out=h_g[c][:, first * PACK : stop * PACK].rearrange("p (c i t) -> p c t i", i=4, t=PACK),
                in_=h_b[c][:, :, first:stop].rearrange("p t (c i) -> p c t i", i=4),
            )

        def scalar_regroups(c):
            return CHUNKS[c] // 2 if c >= NCH - 2 else 0

        def regroup_hidden(c):
            h_g[c] = hq.tile([P, CHUNKS[c] * P * PACK], BF16, name="h_g", align_bytes=64)
            split = CHUNKS[c] - scalar_regroups(c)
            regroup(nc.vector.tensor_copy, c, range(split))
            if split < CHUNKS[c]:
                regroup(nc.scalar.copy, c, range(split, CHUNKS[c]))

        def quantise_hidden(c):
            codes = hq.tile([P, CHUNKS[c] * P], U32, name="h_codes", align_bytes=64)
            scales = hq.tile([P, CHUNKS[c] * P], U8, name="h_scales", align_bytes=64)
            nc.vector.quantize_mx(out=codes.bitcast(FP8X4), scales=scales, in_=h_g[c])
            h_q[c] = (codes, scales)

        st = {}

        def stats_matmuls(c):
            codes, scales = h_q[c]
            for j in range(CHUNKS[c]):
                if j % 2 == 0:
                    st[(c, j // 2)] = psum_s.tile([P, 2, 2 * Z], F32, name="st", tag=("st_0", "st_1")[j // 2])
                tok = slice(j * P, (j + 1) * P)
                nc.tensor.matmul_mx(
                    out=st[(c, j // 2)][:, j % 2, :],
                    lhsT=codes[:, tok].bitcast(FP8X4),
                    lhsT_scale=scales[:, tok],
                    rhs=w2_c.bitcast(FP8X4),
                    rhs_scale=w2_s,
                    start=True,
                    stop=True,
                )

        def chunk_tile(pool, c, label, dtype=F32):
            return pool.tile([P, CHUNKS[c], Z], dtype, name=label)

        def store(dram, c, tile):
            nc.sync.dma_start(out=by_tile(dram)[:, tiles_of(c), :], in_=tile)

        both = {}
        mu = {}
        lv = {}
        std = {}
        inv_sd_p = {}
        diff = {}
        ratio = {}
        dlv = {}
        noise = {}
        sum_sq = const.tile([P, TILES], F32, name="sum_sq")
        sum_ex = const.tile([P, TILES], F32, name="sum_ex")
        sum_df = const.tile([P, TILES], F32, name="sum_df")

        def add_biases(c):
            both[c] = outp.tile([P, 2, CHUNKS[c], Z], F32, name="both")
            for b in range((CHUNKS[c] + 1) // 2):
                tiles = slice(2 * b, min(2 * b + 2, CHUNKS[c]))
                n = tiles.stop - tiles.start
                nc.vector.tensor_tensor(
                    out=both[c][:, :, tiles, :].rearrange("p a j z -> p j a z"),
                    in0=st[(c, b)][:, 0:n, :].rearrange("p j (a z) -> p j a z", a=2),
                    in1=b2_bc.rearrange("p (a z) -> p a z", a=2).unsqueeze(1).to_broadcast([P, n, 2, Z]),
                    op=ALU.add,
                )
            mu[c] = both[c][:, 0, :, :]
            store(mu_out, c, mu[c])

        def clip_logvar(c):
            lv[c] = chunk_tile(outp, c, "lv")
            nc.vector.tensor_scalar(
                out=lv[c], in0=both[c][:, 1, :, :], scalar1=-CLAMP, scalar2=CLAMP, op0=ALU.max, op1=ALU.min
            )
            store(lv_out, c, lv[c])

        def mean_difference(c):
            diff[c] = chunk_tile(scr, c, "diff")
            nc.vector.tensor_tensor(out=diff[c], in0=mu[c], in1=mup_sb[:, tiles_of(c), :], op=ALU.subtract)

        def scale_difference(c):
            ratio[c] = chunk_tile(scr, c, "ratio")
            nc.vector.tensor_tensor(out=ratio[c], in0=diff[c], in1=inv_sd_p[c], op=ALU.mult)

        def logvar_difference(c):
            dlv[c] = chunk_tile(scr, c, "dlv")
            for j in range(CHUNKS[c]):
                tile = FIRST[c] + j
                nc.vector.scalar_tensor_tensor(
                    out=dlv[c][:, j, :],
                    in0=lv[c][:, j, :],
                    scalar=1.0,
                    in1=lvp_sb[:, tile, :],
                    op0=ALU.mult,
                    op1=ALU.subtract,
                    accum_out=sum_df[:, tile : tile + 1],
                )

        def posterior_sd(c):
            std[c] = chunk_tile(scr, c, "std")
            nc.scalar.activation(out=std[c], in_=lv[c], func=ACT.Exp, scale=0.5)

        def prior_inverse_sd(c):
            inv_sd_p[c] = chunk_tile(scr, c, "inv_sd_p")
            nc.scalar.activation(out=inv_sd_p[c], in_=lvp_sb[:, tiles_of(c), :], func=ACT.Exp, scale=-0.5)

        def row_sums(c, func, values, sums, label):
            unread = chunk_tile(scr, c, label, BF16)
            for j in range(CHUNKS[c]):
                tile = FIRST[c] + j
                nc.scalar.activation(
                    out=unread[:, j, :], in_=values[:, j, :], func=func, accum_out=sums[:, tile : tile + 1]
                )

        def sum_exponentials(c):
            row_sums(c, ACT.Exp, dlv[c], sum_ex, "ex_unread")

        def sum_squares(c):
            row_sums(c, ACT.Square, ratio[c], sum_sq, "sq_unread")

        def scale_noise(c):
            noise[c] = chunk_tile(scr, c, "noise")
            nc.vector.tensor_tensor(out=noise[c], in0=std[c], in1=eps_sb[:, tiles_of(c), :], op=ALU.mult)

        z = {}

        def gpsimd_adds(c):
            return 0 if c == NCH - 1 else CHUNKS[c] * 3 // 4

        def add_mean_part(engine, c, first, stop):
            engine.tensor_tensor(
                out=z[c][:, first:stop, :], in0=noise[c][:, first:stop, :], in1=mu[c][:, first:stop, :], op=ALU.add
            )

        def add_mean_gpsimd(c):
            z[c] = chunk_tile(outp, c, "z")
            if gpsimd_adds(c):
                add_mean_part(nc.gpsimd, c, 0, gpsimd_adds(c))

        def add_mean_vector(c):
            if gpsimd_adds(c) < CHUNKS[c]:
                add_mean_part(nc.vector, c, gpsimd_adds(c), CHUNKS[c])
            store(z_out, c, z[c])

        copies = (nc.vector.tensor_copy, nc.scalar.copy)

        def fill_banks():
            while len(banks) - len(emptied) < LEAD and len(banks) < len(fills):
                fill_next()

        def inputs(c, banks_of_chunk, refill=True):
            for q in banks_of_chunk:
                empty_next(nc.scalar.copy, refill)

        for n in range(H_TILES + CHUNKS[0]):
            fill_next()
        b2_bank = psum_s.tile([P, 2 * Z], F32, name="b2_bank", tag="st_1")
        nc.tensor.matmul(b2_bank, lhsT=ones, rhs=b2_row, start=True, stop=True)
        for n in range(3):
            empty_next(copies[n % 2], refill=False)
        quantise_w1(0)
        empty_next(nc.scalar.copy)
        empty_next(nc.vector.tensor_copy)
        empty_next(nc.scalar.copy)
        quantise_w1(1)
        quantise_inputs(0)
        fill_hidden()
        empty_next(nc.scalar.copy)
        w2_bank = psum_s.tile([P, 2, 2 * P], F32, name="w2_bank", tag="st_0")
        transpose_words(nc, w2_bank, ident, [w2_sb.bitcast(F32)[:, w : w + WORDS] for w in (0, WORDS)])
        empty_next(nc.scalar.copy)
        quantise_inputs(1)
        b2_bc = const.tile([P, 2 * Z], F32, name="b2_bc")
        nc.scalar.copy(out=b2_bc, in_=b2_bank)
        empty_next(nc.scalar.copy)
        w2_g = const.tile([P, 2 * Z * PACK], BF16, name="w2_g", align_bytes=64)
        w2_c = const.tile([P, 2 * Z], U32, name="w2_c", align_bytes=64)
        w2_s = const.tile([P, 2 * Z], U8, name="w2_s", align_bytes=64)

        for i in range(NCH + 1):
            last = CHUNKS[i + 2] - 1 if i + 2 < NCH else 0
            if i >= 1 and i + 5 < NCH:
                load_chunk(i + 5)
                load_prior(range(i + 4, i + 5))
            elif i + 4 < NCH and i >= 1:
                load_prior(range(i + 4, i + 5))
            if i < NCH:
                for b in range(hidden_banks(i)):
                    relu_bank(i, b)
                    if i >= 1 and b == 0:
                        if i >= 2:
                            fill_hidden()
                        fill_banks()
            if i >= 1:
                add_biases(i - 1)
            if 2 <= i < NCH:
                scale_difference(i - 2)
            if i >= 1:
                clip_logvar(i - 1)
            if i >= 2:
                add_mean_vector(i - 2)
            if i >= 1:
                mean_difference(i - 1)
            if i + 2 < NCH:
                if i > 0:
                    inputs(i + 2, range(0, 1))
                if i > 0:
                    fill_hidden()
                inputs(i + 2, range(1, last), refill=False)
            if i >= 1:
                fill_hidden()
            if i >= 1:
                posterior_sd(i - 1)
            if i < NCH:
                regroup_hidden(i)
            if i == 0:
                copy_grouped(nc.vector.tensor_copy, w2_bank, w2_g.bitcast(F32))
                quantise_hidden(0)
                nc.vector.quantize_mx(out=w2_c.bitcast(FP8X4), scales=w2_s, in_=w2_g)
            if i >= 1:
                logvar_difference(i - 1)
            if 1 <= i < NCH:
                quantise_hidden(i)
            if i == 0:
                fill_hidden()
            if i < NCH:
                stats_matmuls(i)
            if i == 0:
                for n in range(LEAD - 1):
                    fill_next()
            if i + 2 < NCH:
                inputs(i + 2, range(last, last + 1), refill=False)
            if i >= 1:
                scale_noise(i - 1)
            if i >= NCH - 1:
                scale_difference(i - 1)
            if i + 2 < NCH:
                quantise_inputs(i + 2)
            if i >= 1:
                add_mean_gpsimd(i - 1)
            if i == NCH:
                add_mean_vector(i - 1)
            if 2 <= i < NCH:
                sum_exponentials(i - 2)
                sum_squares(i - 2)
            if i >= NCH - 1:
                sum_exponentials(i - 1)
                sum_squares(i - 1)
            if i < NCH:
                prior_inverse_sd(i)

        linear = const.tile([P, TILES], F32, name="linear")
        nc.vector.tensor_scalar(out=linear, in0=sum_df, scalar1=-0.5, scalar2=-0.5 * Z, op0=ALU.mult, op1=ALU.add)
        partial = const.tile([P, TILES], F32, name="partial")
        nc.vector.scalar_tensor_tensor(
            out=partial, in0=sum_ex, scalar=0.5, in1=linear, op0=ALU.mult, op1=ALU.add
        )
        kl = const.tile([P, TILES], F32, name="kl")
        nc.vector.scalar_tensor_tensor(out=kl, in0=sum_sq, scalar=0.5, in1=partial, op0=ALU.mult, op1=ALU.add)
        nc.sync.dma_start(out=kl_out.rearrange("(p j) -> p j", j=TILES), in_=kl)
